import numpy as np
import ml_dtypes


def mxq(x, axis, fmt="e4m3"):
    dtype, down = {"e4m3": (ml_dtypes.float8_e4m3fn, 7), "e5m2": (ml_dtypes.float8_e5m2, 14)}[fmt]
    v = np.moveaxis(np.asarray(x, np.float32).astype(ml_dtypes.bfloat16).astype(np.float64), axis, -1)
    blocks = v.reshape(v.shape[:-1] + (-1, 32))
    amax = np.abs(blocks).max(-1, keepdims=True)
    byte = np.maximum(np.where(amax > 0, np.frexp(amax)[1] - 1 + 127, 0) - down, 1)
    scale = np.exp2(byte - 127.0)
    codes = (blocks / scale).astype(np.float32).astype(dtype).astype(np.float64)
    return np.moveaxis((codes * scale).reshape(v.shape), -1, axis)


WIDE = False


def mx_kscale(k):
    if not WIDE:
        return np.ones(k)
    levels = np.array([10, -10, 5, -5, 0])
    a = np.random.permutation(np.resize(levels, k // 512 * 4)).reshape(k // 512, 4)
    idx = np.arange(k)
    return np.exp2(a[idx // 512, idx % 128 // 32])


BF16 = ml_dtypes.bfloat16


def bf(x):
    return np.asarray(x, np.float32).astype(BF16)


def f64(x):
    return np.asarray(x).astype(np.float64)


B, N, F, U, S = 32, 512, 128, 128, 2
C = S * (F + U)


def sigmoid(v):
    return 1.0 / (1.0 + np.exp(-v))


def random_walk():
    a = np.random.uniform(size=(N, N))
    return a / a.sum(axis=1, keepdims=True) * np.sqrt(N)


def setup_inputs():
    s = mx_kscale(N)
    return {"r_prev": bf(sigmoid(np.random.standard_normal((B, U, N))) * np.random.standard_normal((B, U, N)) * s),
            "h_diff": bf(np.random.standard_normal((B, N, S * F))),
            "u": bf(sigmoid(np.random.standard_normal((B, N, U)))),
            "state": bf(np.random.standard_normal((B, U * N))),
            "support0": bf(random_walk() / s[None, :]),
            "support1": bf(random_walk() / s[None, :]),
            "c_kernel": bf(np.random.standard_normal((C, U)) / np.sqrt(C))}


def diffuse(xq, supq):
    return np.concatenate([(xq @ sq.T) for sq in supq], axis=1)


def reference(r_prev, h_diff, u, state, support0, support1, c_kernel):
    supq = (mxq(f64(support0), 1, "e4m3"), mxq(f64(support1), 1, "e4m3"))
    c_state = diffuse(mxq(f64(r_prev), 2, "e4m3"), supq).transpose(0, 2, 1)
    hc = np.concatenate([f64(h_diff), c_state], axis=-1)
    c = np.tanh(mxq(hc, 2, "e4m3") @ mxq(f64(c_kernel), 0, "e4m3"))
    prev_t = f64(state).reshape(B, U, N).transpose(0, 2, 1)
    ug = f64(u)
    z = ug * prev_t + (1.0 - ug) * c
    return z.reshape(B, U * N)

@@ -1,0 +1,358 @@
+from contextlib import ExitStack
+
+import concourse.mybir as mybir
+from concourse.masks import make_identity
+
+F32 = mybir.dt.float32
+BF16 = mybir.dt.bfloat16
+U32 = mybir.dt.uint32
+U8 = mybir.dt.uint8
+I32 = mybir.dt.int32
+FP8X4 = mybir.dt.float8_e4m3fn_x4
+TANH = mybir.ActivationFunctionType.Tanh
+ALU = mybir.AluOpType
+
+P = 128
+PAIRS = 16
+LOAD_BUFS = 6
+MANUAL = True
+
+FLOPS = 2 * 32 * 256 * 512 * 512 + 2 * 32 * 512 * 512 * 128
+
+
+def tile_gcrnncell_pb_t_kernel(tc, r_prev, h_diff, u, state, support0, support1, c_kernel, out):
+    nc = tc.nc
+    r_rows = r_prev.rearrange("b k n -> (b k) n")
+    with ExitStack() as ctx:
+        const = ctx.enter_context(tc.tile_pool(name="const", bufs=1))
+        loads = ctx.enter_context(tc.tile_pool(name="loads", bufs=LOAD_BUFS))
+        work = ctx.enter_context(tc.tile_pool(name="work", bufs=2))
+        psum = ctx.enter_context(tc.psum_pool(name="psum", bufs=2))
+        if MANUAL:
+            ctx.enter_context(tc.manual_schedule())
+
+        r_raw = {}
+        h_raw = {}
+        s_raw = {}
+        u_raw = {}
+        bank_r = {}
+        bank_x = {}
+        bank_s = {}
+        bank_y = {}
+        bank_o = {}
+        r_grp = {}
+        r_mx = {}
+        x_grp = {}
+        x_mx = {}
+        y_grp = {}
+        y_mx = {}
+        cand = {}
+        mix = {}
+
+        def ok(pair):
+            return 0 <= pair < PAIRS
+
+        def load_r(pair):
+            if not ok(pair):
+                return
+            t = loads.tile([P, 1024], BF16, name="r_raw", tag="r_raw")
+            nc.sync.dma_start(out=t[:], in_=r_rows[256 * pair : 256 * pair + 256, :].rearrange("(c h) n -> c (h n)", h=2))
+            r_raw[pair] = t
+
+        def load_h(pair):
+            if not ok(pair):
+                return
+            t = loads.tile([P, 2048], BF16, name="h_raw", tag="h_raw")
+            nc.sync.dma_start(
+                out=t[:].rearrange("p (b f) -> p b f", b=2),
+                in_=h_diff[2 * pair : 2 * pair + 2].rearrange("b (p j) c -> p b (j c)", j=4),
+            )
+            h_raw[pair] = t
+
+        def load_s(pair):
+            if not ok(pair):
+                return
+            t = loads.tile([P, 1024], BF16, name="s_raw", tag="s_raw")
+            nc.sync.dma_start(
+                out=t[:].rearrange("k (b n) -> k b n", b=2),
+                in_=state[2 * pair : 2 * pair + 2].rearrange("b (k n) -> k b n", n=512),
+            )
+            s_raw[pair] = t
+
+        def load_u(pair):
+            if not ok(pair):
+                return
+            t = loads.tile([P, 1024], BF16, name="u_raw", tag="u_raw")
+            nc.sync.dma_start(
+                out=t[:].rearrange("p (b f) -> p b f", b=2),
+                in_=u[2 * pair : 2 * pair + 2].rearrange("b (p j) k -> p b (j k)", j=4),
+            )
+            u_raw[pair] = t
+
+        def tr_r(pair):
+            if not ok(pair):
+                return
+            bank = psum.tile([P, 512], F32, name="bank_r", tag="bank_r", bufs=1)
+            words = r_raw[pair][:].bitcast(F32)
+            for g in range(4):
+                nc.tensor.transpose(out=bank[:, 128 * g : 128 * g + 128], in_=words[:, 128 * g : 128 * g + 128], identity=ident[:])
+            bank_r[pair] = bank
+
+        def ev_r(pair):
+            if not ok(pair):
+                return
+            grp = work.tile([P, 1024], BF16, name="r_grp", tag="r_grp", align_bytes=64)
+            nc.scalar.copy(
+                out=grp[:].bitcast(F32).rearrange("w (h c t) -> w h c t", h=2, t=2),
+                in_=bank_r[pair][:].rearrange("w (h t c) -> w h c t", h=2, t=2),
+            )
+            r_grp[pair] = grp
+
+        def q_r(pair):
+            if not ok(pair):
+                return
+            codes = work.tile([P, 256], U32, name="r_codes", tag="r_codes", bufs=3, align_bytes=64)
+            scales = work.tile([P, 256], U8, name="r_scales", tag="r_scales", bufs=3, align_bytes=64)
+            nc.vector.quantize_mx(out=codes[:].bitcast(FP8X4), scales=scales[:], in_=r_grp[pair][:])
+            r_mx[pair] = (codes, scales)
+
+        def tr_x(pair, bs):
+            if not ok(pair):
+                return
+            bank = psum.tile([P, 512], F32, name="bank_x", tag="bank_x")
+            view = h_raw[pair][:].bitcast(F32).rearrange("p (b a x s) -> p b a x s", b=2, a=2, s=2)
+            for a in range(2):
+                for s in range(2):
+                    g = 2 * a + s
+                    nc.tensor.transpose(out=bank[:, 128 * g : 128 * g + 128], in_=view[:, bs, a, :, s], identity=ident[:])
+            bank_x[(pair, bs)] = bank
+
+        def ev_x(pair, bs):
+            if not ok(pair):
+                return
+            if bs == 0:
+                x_grp[pair] = work.tile([P, 2048], BF16, name="x_grp", tag="x_grp", align_bytes=64)
+            nc.scalar.copy(
+                out=x_grp[pair][:].bitcast(F32)[:, 512 * bs : 512 * bs + 512].rearrange("x (a p s) -> x a p s", a=2, s=2),
+                in_=bank_x[(pair, bs)][:].rearrange("x (a s p) -> x a p s", a=2, s=2),
+            )
+
+        def q_x(pair):
+            if not ok(pair):
+                return
+            codes = work.tile([P, 512], U32, name="x_codes", tag="x_codes", bufs=3, align_bytes=64)
+            scales = work.tile([P, 512], U8, name="x_scales", tag="x_scales", bufs=3, align_bytes=64)
+            nc.vector.quantize_mx(out=codes[:].bitcast(FP8X4), scales=scales[:], in_=x_grp[pair][:])
+            x_mx[pair] = (codes, scales)
+
+        def mx1(pair, j):
+            if not ok(pair):
+                return
+            bank = psum.tile([P, 512], F32, name="bank_y", tag="bank_y")
+            codes, scales = r_mx[pair]
+            for h in range(2):
+                nc.tensor.matmul_mx(
+                    out=bank[:, 256 * h : 256 * h + 256],
+                    lhsT=codes[:, 128 * h : 128 * h + 128].bitcast(FP8X4),
+                    lhsT_scale=scales[:, 128 * h : 128 * h + 128],
+                    rhs=sup_codes[:, 256 * j : 256 * j + 256].bitcast(FP8X4),
+                    rhs_scale=sup_scales[:, 256 * j : 256 * j + 256],
+                    start=True,
+                    stop=True,
+                )
+            bank_y[(pair, j)] = bank
+
+        def ev_y(pair, j):
+            if not ok(pair):
+                return
+            if j == 0:
+                y_grp[pair] = work.tile([P, 2048], BF16, name="y_grp", tag="y_grp", align_bytes=64)
+            nc.scalar.copy(
+                out=y_grp[pair][:, 512 * j : 512 * j + 512].rearrange("c (p i h) -> c p i h", i=2, h=2),
+                in_=bank_y[(pair, j)][:].rearrange("c (h i p) -> c p i h", h=2, i=2),
+            )
+
+        def q_y(pair):
+            if not ok(pair):
+                return
+            codes = work.tile([P, 512], U32, name="y_codes", tag="y_codes", align_bytes=64)
+            scales = work.tile([P, 512], U8, name="y_scales", tag="y_scales", align_bytes=64)
+            nc.vector.quantize_mx(out=codes[:].bitcast(FP8X4), scales=scales[:], in_=y_grp[pair][:])
+            y_mx[pair] = (codes, scales)
+
+        def mx2(pair, bs):
+            if not ok(pair):
+                return
+            bank = psum.tile([P, 512], F32, name="bank_o", tag="bank_o")
+            xc, xs = x_mx[pair]
+            yc, ys = y_mx[pair]
+            for j in range(4):
+                xcol = 256 * bs + 128 * (j // 2)
+                kx = 128 * (j % 2)
+                ky = 128 * (2 + bs)
+                nc.tensor.matmul_mx(
+                    out=bank[:, 128 * j : 128 * j + 128],
+                    lhsT=xc[:, xcol : xcol + 128].bitcast(FP8X4),
+                    lhsT_scale=xs[:, xcol : xcol + 128],
+                    rhs=ck_codes[:, kx : kx + 128].bitcast(FP8X4),
+                    rhs_scale=ck_scales[:, kx : kx + 128],
+                    start=True,
+                    stop=False,
+                )
+                nc.tensor.matmul_mx(
+                    out=bank[:, 128 * j : 128 * j + 128],
+                    lhsT=yc[:, 128 * j : 128 * j + 128].bitcast(FP8X4),
+                    lhsT_scale=ys[:, 128 * j : 128 * j + 128],
+                    rhs=ck_codes[:, ky : ky + 128].bitcast(FP8X4),
+                    rhs_scale=ck_scales[:, ky : ky + 128],
+                    start=False,
+                    stop=True,
+                )
+            bank_o[(pair, bs)] = bank
+
+        def tanh(pair, bs):
+            if not ok(pair):
+                return
+            if bs == 0:
+                cand[pair] = work.tile([P, 1024], F32, name="cand", tag="cand")
+            nc.scalar.activation(out=cand[pair][:, 512 * bs : 512 * bs + 512], in_=bank_o[(pair, bs)][:], func=TANH)
+
+        def tr_s(pair):
+            if not ok(pair):
+                return
+            bank = psum.tile([P, 512], F32, name="bank_s", tag="bank_s", bufs=1)
+            view = s_raw[pair][:].bitcast(F32).rearrange("k (b x s) -> k b x s", b=2, s=2)
+            for b in range(2):
+                for s in range(2):
+                    g = 2 * b + s
+                    nc.tensor.transpose(out=bank[:, 128 * g : 128 * g + 128], in_=view[:, b, :, s], identity=ident[:])
+            bank_s[pair] = bank
+
+        def blend_d(pair):
+            if not ok(pair):
+                return
+            t = work.tile([P, 1024], F32, name="mix", tag="mix", bufs=3)
+            nc.vector.tensor_tensor(
+                out=t[:].rearrange("p (g e k) -> p g e k", g=4, e=2),
+                in0=bank_s[pair][:].bitcast(BF16).rearrange("p (g k e) -> p g e k", g=4, e=2),
+                in1=cand[pair][:].rearrange("p (g e k) -> p g e k", g=4, e=2),
+                op=ALU.subtract,
+            )
+            mix[pair] = t
+
+        def blend_ez(pair):
+            if not ok(pair):
+                return
+            t = mix[pair]
+            nc.vector.tensor_tensor(out=t[:], in0=t[:], in1=u_raw[pair][:], op=ALU.mult)
+            nc.vector.tensor_tensor(out=t[:], in0=t[:], in1=cand[pair][:], op=ALU.add)
+            nc.sync.dma_start(
+                out=out[2 * pair : 2 * pair + 2].rearrange("b (p f) -> p b f", p=P),
+                in_=t[:].rearrange("p (b f) -> p b f", b=2),
+            )
+
+        ident = const.tile([P, P], F32, name="ident")
+        make_identity(nc, ident[:])
+        warm = const.tile([P, 2], F32, name="warm")
+        nc.vector.memset(warm[:], 0.0)
+        nc.scalar.activation(out=warm[:, 1:2], in_=warm[:, 0:1], func=TANH)
+
+        ck_raw = const.tile([P, 2048], BF16, name="ck_raw")
+        nc.vector.memset(ck_raw[:].bitcast(I32), 0)
+        ck_h = c_kernel[0:256, :].rearrange("(q t) u -> q (t u)", t=4)
+        ck_c = c_kernel[256:512, :].rearrange("(i q h) u -> q i (h u)", i=2, h=2)
+
+        sup_raw = []
+        load_r(0)
+        for i, sup in enumerate((support0, support1)):
+            t = const.tile([P, 2048], BF16, name="sup_raw%d" % i)
+            nc.sync.dma_start(out=t[:], in_=sup.rearrange("(p j) n -> p (j n)", j=4))
+            sup_raw.append(t)
+        for step in range(-1, LOAD_BUFS + 2):
+            if 0 <= step + 1 < LOAD_BUFS:
+                load_h(step + 1)
+            if 0 < step + 2 < LOAD_BUFS:
+                load_r(step + 2)
+            if 0 <= step - 1 < LOAD_BUFS:
+                load_s(step - 1)
+            if 0 <= step - 2 < LOAD_BUFS:
+                load_u(step - 2)
+            if step == 0:
+                nc.sync.dma_start(out=ck_raw[0:64, 0:512], in_=ck_h)
+                nc.sync.dma_start(out=ck_raw[64:128, 512:1024], in_=ck_h)
+                nc.sync.dma_start(out=ck_raw[0:64, 1024:1536].rearrange("q (i f) -> q i f", i=2), in_=ck_c)
+                nc.sync.dma_start(out=ck_raw[64:128, 1536:2048].rearrange("q (i f) -> q i f", i=2), in_=ck_c)
+
+        ck_grp = const.tile([P, 2048], BF16, name="ck_grp", align_bytes=64)
+        ck_codes = const.tile([P, 512], U32, name="ck_codes", align_bytes=64)
+        ck_scales = const.tile([P, 512], U8, name="ck_scales", align_bytes=64)
+        sup_grp = const.tile([P, 4096], BF16, name="sup_grp", align_bytes=64)
+        sup_codes = const.tile([P, 1024], U32, name="sup_codes", align_bytes=64)
+        sup_scales = const.tile([P, 1024], U8, name="sup_scales", align_bytes=64)
+
+        def prepare_kernel():
+            nc.vector.tensor_copy(
+                out=ck_grp[:].rearrange("p (v u t) -> p v u t", v=4, t=4),
+                in_=ck_raw[:].rearrange("p (v t u) -> p v u t", v=4, t=4),
+            )
+            nc.vector.quantize_mx(out=ck_codes[:].bitcast(FP8X4), scales=ck_scales[:], in_=ck_grp[:])
+
+        def prepare_supports():
+            grp_words = sup_grp[:].bitcast(F32).rearrange("w (a b i f) -> w a b i f", a=2, b=2, i=2)
+            for i in range(2):
+                words = sup_raw[i][:].bitcast(F32)
+                for a in range(2):
+                    bank = psum.tile([P, 512], F32, name="bank_c", tag=("bank_x" if i == 0 else "bank_y"))
+                    for g in range(4):
+                        col = 512 * a + 128 * g
+                        nc.tensor.transpose(out=bank[:, 128 * g : 128 * g + 128], in_=words[:, col : col + 128], identity=ident[:])
+                    dst = grp_words[:, a, :, i, :].rearrange("w b (p t) -> w b p t", t=2)
+                    src = bank[:].rearrange("w (b t p) -> w b p t", b=2, t=2)
+                    if a == 0:
+                        nc.vector.tensor_copy(out=dst, in_=src)
+                    else:
+                        nc.scalar.copy(out=dst, in_=src)
+            for a in range(2):
+                nc.vector.quantize_mx(
+                    out=sup_codes[:, 512 * a : 512 * a + 512].bitcast(FP8X4),
+                    scales=sup_scales[:, 512 * a : 512 * a + 512],
+                    in_=sup_grp[:, 2048 * a : 2048 * a + 2048],
+                )
+
+        for step in range(-2, PAIRS + 2):
+            blend_d(step - 2)
+            ev_y(step - 1, 2)
+            ev_y(step - 1, 3)
+            tr_r(step + 2)
+            tr_x(step + 1, 0)
+            tr_x(step + 1, 1)
+            tr_s(step - 1)
+            q_y(step - 1)
+            ev_r(step + 2)
+            ev_x(step + 1, 0)
+            ev_x(step + 1, 1)
+            mx1(step, 0)
+            mx1(step, 1)
+            mx2(step - 1, 0)
+            mx2(step - 1, 1)
+            ev_y(step, 0)
+            ev_y(step, 1)
+            mx1(step, 2)
+            mx1(step, 3)
+            tanh(step - 1, 0)
+            tanh(step - 1, 1)
+            blend_ez(step - 2)
+            q_r(step + 2)
+            q_x(step + 1)
+            if step + 2 >= 0:
+                load_r(step + 2 + LOAD_BUFS)
+            if step + 1 >= 0:
+                load_h(step + 1 + LOAD_BUFS)
+            if step - 1 >= 0:
+                load_s(step - 1 + LOAD_BUFS)
+            if step - 2 >= 0:
+                load_u(step - 2 + LOAD_BUFS)
+            if step == -2:
+                prepare_supports()
+            if step == -1:
+                prepare_kernel()

@@ -137,13 +137,19 @@ def tile_gcrnncell_pb_t_kernel(tc, r_prev, h_diff, u, state, support0, support1,
                 in_=bank_x[(pair, bs)][:].rearrange("x (a s p) -> x a p s", a=2, s=2),
             )
 
-        def q_x(pair):
+        def q_x(pair, bs):
             if not ok(pair):
                 return
-            codes = work.tile([P, 512], U32, name="x_codes", tag="x_codes", bufs=3, align_bytes=64)
-            scales = work.tile([P, 512], U8, name="x_scales", tag="x_scales", bufs=3, align_bytes=64)
-            nc.vector.quantize_mx(out=codes[:].bitcast(FP8X4), scales=scales[:], in_=x_grp[pair][:])
-            x_mx[pair] = (codes, scales)
+            if bs == 0:
+                codes = work.tile([P, 512], U32, name="x_codes", tag="x_codes", bufs=3, align_bytes=64)
+                scales = work.tile([P, 512], U8, name="x_scales", tag="x_scales", bufs=3, align_bytes=64)
+                x_mx[pair] = (codes, scales)
+            codes, scales = x_mx[pair]
+            nc.vector.quantize_mx(
+                out=codes[:, 256 * bs : 256 * bs + 256].bitcast(FP8X4),
+                scales=scales[:, 256 * bs : 256 * bs + 256],
+                in_=x_grp[pair][:, 1024 * bs : 1024 * bs + 1024],
+            )
 
         def mx1(pair, j):
             if not ok(pair):
@@ -240,11 +246,16 @@ def tile_gcrnncell_pb_t_kernel(tc, r_prev, h_diff, u, state, support0, support1,
             )
             mix[pair] = t
 
-        def blend_ez(pair):
+        def blend_e(pair):
             if not ok(pair):
                 return
             t = mix[pair]
             nc.vector.tensor_tensor(out=t[:], in0=t[:], in1=u_raw[pair][:], op=ALU.mult)
+
+        def blend_z(pair):
+            if not ok(pair):
+                return
+            t = mix[pair]
             nc.vector.tensor_tensor(out=t[:], in0=t[:], in1=cand[pair][:], op=ALU.add)
             nc.sync.dma_start(
                 out=out[2 * pair : 2 * pair + 2].rearrange("b (p f) -> p b f", p=P),
@@ -320,30 +331,32 @@ def tile_gcrnncell_pb_t_kernel(tc, r_prev, h_diff, u, state, support0, support1,
                 )
 
         for step in range(-2, PAIRS + 2):
-            blend_d(step - 2)
-            ev_y(step - 1, 2)
-            ev_y(step - 1, 3)
+            q_y(step - 1)
             tr_r(step + 2)
             tr_x(step + 1, 0)
-            tr_x(step + 1, 1)
-            tr_s(step - 1)
-            q_y(step - 1)
+            blend_d(step - 2)
             ev_r(step + 2)
             ev_x(step + 1, 0)
-            ev_x(step + 1, 1)
             mx1(step, 0)
             mx1(step, 1)
             mx2(step - 1, 0)
-            mx2(step - 1, 1)
             ev_y(step, 0)
             ev_y(step, 1)
+            tanh(step - 1, 0)
+            q_r(step + 2)
+            blend_e(step - 2)
+            q_x(step + 1, 0)
+            tr_x(step + 1, 1)
+            tr_s(step - 1)
+            ev_x(step + 1, 1)
             mx1(step, 2)
             mx1(step, 3)
-            tanh(step - 1, 0)
+            mx2(step - 1, 1)
+            ev_y(step, 2)
+            ev_y(step, 3)
             tanh(step - 1, 1)
-            blend_ez(step - 2)
-            q_r(step + 2)
-            q_x(step + 1)
+            blend_z(step - 2)
+            q_x(step + 1, 1)
             if step + 2 >= 0:
                 load_r(step + 2 + LOAD_BUFS)
             if step + 1 >= 0:

@@ -16,6 +16,7 @@ P = 128
 PAIRS = 16
 LOAD_BUFS = 6
 MANUAL = True
+POOL_TAIL = 1
 
 FLOPS = 2 * 32 * 256 * 512 * 512 + 2 * 32 * 512 * 512 * 128
 
@@ -132,10 +133,12 @@ def tile_gcrnncell_pb_t_kernel(tc, r_prev, h_diff, u, state, support0, support1,
                 return
             if bs == 0:
                 x_grp[pair] = work.tile([P, 2048], BF16, name="x_grp", tag="x_grp", align_bytes=64)
-            nc.scalar.copy(
-                out=x_grp[pair][:].bitcast(F32)[:, 512 * bs : 512 * bs + 512].rearrange("x (a p s) -> x a p s", a=2, s=2),
-                in_=bank_x[(pair, bs)][:].rearrange("x (a s p) -> x a p s", a=2, s=2),
-            )
+            dst = x_grp[pair][:].bitcast(F32)[:, 512 * bs : 512 * bs + 512].rearrange("x (a p s) -> x a p s", a=2, s=2)
+            src = bank_x[(pair, bs)][:].rearrange("x (a s p) -> x a p s", a=2, s=2)
+            if bs == 0:
+                nc.scalar.copy(out=dst, in_=src)
+            else:
+                nc.vector.tensor_copy(out=dst, in_=src)
 
         def q_x(pair, bs):
             if not ok(pair):
@@ -220,7 +223,7 @@ def tile_gcrnncell_pb_t_kernel(tc, r_prev, h_diff, u, state, support0, support1,
             if not ok(pair):
                 return
             if bs == 0:
-                cand[pair] = work.tile([P, 1024], F32, name="cand", tag="cand")
+                cand[pair] = work.tile([P, 1024], F32, name="cand", tag="cand", bufs=3)
             nc.scalar.activation(out=cand[pair][:, 512 * bs : 512 * bs + 512], in_=bank_o[(pair, bs)][:], func=TANH)
 
         def tr_s(pair):
@@ -237,7 +240,7 @@ def tile_gcrnncell_pb_t_kernel(tc, r_prev, h_diff, u, state, support0, support1,
         def blend_d(pair):
             if not ok(pair):
                 return
-            t = work.tile([P, 1024], F32, name="mix", tag="mix", bufs=3)
+            t = work.tile([P, 1024], F32, name="mix", tag="mix", bufs=4)
             nc.vector.tensor_tensor(
                 out=t[:].rearrange("p (g e k) -> p g e k", g=4, e=2),
                 in0=bank_s[pair][:].bitcast(BF16).rearrange("p (g k e) -> p g e k", g=4, e=2),
@@ -256,7 +259,10 @@ def tile_gcrnncell_pb_t_kernel(tc, r_prev, h_diff, u, state, support0, support1,
             if not ok(pair):
                 return
             t = mix[pair]
-            nc.vector.tensor_tensor(out=t[:], in0=t[:], in1=cand[pair][:], op=ALU.add)
+            if pair < PAIRS - POOL_TAIL:
+                nc.gpsimd.tensor_tensor(out=t[:], in0=t[:], in1=cand[pair][:], op=ALU.add)
+            else:
+                nc.vector.tensor_tensor(out=t[:], in0=t[:], in1=cand[pair][:], op=ALU.add)
             nc.sync.dma_start(
                 out=out[2 * pair : 2 * pair + 2].rearrange("b (p f) -> p b f", p=P),
                 in_=t[:].rearrange("p (b f) -> p b f", b=2),
@@ -279,20 +285,19 @@ def tile_gcrnncell_pb_t_kernel(tc, r_prev, h_diff, u, state, support0, support1,
             t = const.tile([P, 2048], BF16, name="sup_raw%d" % i)
             nc.sync.dma_start(out=t[:], in_=sup.rearrange("(p j) n -> p (j n)", j=4))
             sup_raw.append(t)
-        for step in range(-1, LOAD_BUFS + 2):
-            if 0 <= step + 1 < LOAD_BUFS:
-                load_h(step + 1)
-            if 0 < step + 2 < LOAD_BUFS:
-                load_r(step + 2)
-            if 0 <= step - 1 < LOAD_BUFS:
-                load_s(step - 1)
+        nc.sync.dma_start(out=ck_raw[0:64, 0:512], in_=ck_h)
+        nc.sync.dma_start(out=ck_raw[64:128, 512:1024], in_=ck_h)
+        nc.sync.dma_start(out=ck_raw[0:64, 1024:1536].rearrange("q (i f) -> q i f", i=2), in_=ck_c)
+        nc.sync.dma_start(out=ck_raw[64:128, 1536:2048].rearrange("q (i f) -> q i f", i=2), in_=ck_c)
+        for step in range(0, LOAD_BUFS + 3):
+            if 0 <= step < LOAD_BUFS:
+                load_h(step)
+            if 0 < step + 1 < LOAD_BUFS:
+                load_r(step + 1)
             if 0 <= step - 2 < LOAD_BUFS:
-                load_u(step - 2)
-            if step == 0:
-                nc.sync.dma_start(out=ck_raw[0:64, 0:512], in_=ck_h)
-                nc.sync.dma_start(out=ck_raw[64:128, 512:1024], in_=ck_h)
-                nc.sync.dma_start(out=ck_raw[0:64, 1024:1536].rearrange("q (i f) -> q i f", i=2), in_=ck_c)
-                nc.sync.dma_start(out=ck_raw[64:128, 1536:2048].rearrange("q (i f) -> q i f", i=2), in_=ck_c)
+                load_s(step - 2)
+            if 0 <= step - 3 < LOAD_BUFS:
+                load_u(step - 3)
 
         ck_grp = const.tile([P, 2048], BF16, name="ck_grp", align_bytes=64)
         ck_codes = const.tile([P, 512], U32, name="ck_codes", align_bytes=64)
@@ -330,42 +335,41 @@ def tile_gcrnncell_pb_t_kernel(tc, r_prev, h_diff, u, state, support0, support1,
                     in_=sup_grp[:, 2048 * a : 2048 * a + 2048],
                 )
 
-        for step in range(-2, PAIRS + 2):
+        for step in range(-1, PAIRS + 3):
             q_y(step - 1)
-            tr_r(step + 2)
-            tr_x(step + 1, 0)
+            blend_e(step - 3)
+            blend_z(step - 3)
+            tr_r(step + 1)
+            tr_s(step - 2)
             blend_d(step - 2)
-            ev_r(step + 2)
-            ev_x(step + 1, 0)
+            ev_r(step + 1)
             mx1(step, 0)
             mx1(step, 1)
             mx2(step - 1, 0)
             ev_y(step, 0)
             ev_y(step, 1)
             tanh(step - 1, 0)
-            q_r(step + 2)
-            blend_e(step - 2)
-            q_x(step + 1, 0)
-            tr_x(step + 1, 1)
-            tr_s(step - 1)
-            ev_x(step + 1, 1)
+            tr_x(step, 0)
+            tr_x(step, 1)
+            ev_x(step, 0)
+            ev_x(step, 1)
+            q_r(step + 1)
+            q_x(step, 0)
+            q_x(step, 1)
             mx1(step, 2)
             mx1(step, 3)
             mx2(step - 1, 1)
             ev_y(step, 2)
             ev_y(step, 3)
             tanh(step - 1, 1)
-            blend_z(step - 2)
-            q_x(step + 1, 1)
-            if step + 2 >= 0:
-                load_r(step + 2 + LOAD_BUFS)
             if step + 1 >= 0:
-                load_h(step + 1 + LOAD_BUFS)
-            if step - 1 >= 0:
-                load_s(step - 1 + LOAD_BUFS)
+                load_r(step + 1 + LOAD_BUFS)
+            if step >= 0:
+                load_h(step + LOAD_BUFS)
             if step - 2 >= 0:
-                load_u(step - 2 + LOAD_BUFS)
-            if step == -2:
-                prepare_supports()
+                load_s(step - 2 + LOAD_BUFS)
+            if step - 3 >= 0:
+                load_u(step - 3 + LOAD_BUFS)
             if step == -1:
+                prepare_supports()
                 prepare_kernel()

@@ -14,9 +14,10 @@ ALU = mybir.AluOpType
 
 P = 128
 PAIRS = 16
-LOAD_BUFS = 6
+FETCH = 3
 MANUAL = True
-POOL_TAIL = 1
+RL = 1
+XL = 0
 
 FLOPS = 2 * 32 * 256 * 512 * 512 + 2 * 32 * 512 * 512 * 128
 
@@ -26,7 +27,7 @@ def tile_gcrnncell_pb_t_kernel(tc, r_prev, h_diff, u, state, support0, support1,
     r_rows = r_prev.rearrange("b k n -> (b k) n")
     with ExitStack() as ctx:
         const = ctx.enter_context(tc.tile_pool(name="const", bufs=1))
-        loads = ctx.enter_context(tc.tile_pool(name="loads", bufs=LOAD_BUFS))
+        loads = ctx.enter_context(tc.tile_pool(name="loads", bufs=FETCH + 2))
         work = ctx.enter_context(tc.tile_pool(name="work", bufs=2))
         psum = ctx.enter_context(tc.psum_pool(name="psum", bufs=2))
         if MANUAL:
@@ -83,7 +84,7 @@ def tile_gcrnncell_pb_t_kernel(tc, r_prev, h_diff, u, state, support0, support1,
         def load_u(pair):
             if not ok(pair):
                 return
-            t = loads.tile([P, 1024], BF16, name="u_raw", tag="u_raw")
+            t = loads.tile([P, 1024], BF16, name="u_raw", tag="u_raw", bufs=FETCH + 4)
             nc.sync.dma_start(
                 out=t[:].rearrange("p (b f) -> p b f", b=2),
                 in_=u[2 * pair : 2 * pair + 2].rearrange("b (p j) k -> p b (j k)", j=4),
@@ -133,12 +134,10 @@ def tile_gcrnncell_pb_t_kernel(tc, r_prev, h_diff, u, state, support0, support1,
                 return
             if bs == 0:
                 x_grp[pair] = work.tile([P, 2048], BF16, name="x_grp", tag="x_grp", align_bytes=64)
-            dst = x_grp[pair][:].bitcast(F32)[:, 512 * bs : 512 * bs + 512].rearrange("x (a p s) -> x a p s", a=2, s=2)
-            src = bank_x[(pair, bs)][:].rearrange("x (a s p) -> x a p s", a=2, s=2)
-            if bs == 0:
-                nc.scalar.copy(out=dst, in_=src)
-            else:
-                nc.vector.tensor_copy(out=dst, in_=src)
+            nc.scalar.copy(
+                out=x_grp[pair][:].bitcast(F32)[:, 512 * bs : 512 * bs + 512].rearrange("x (a p s) -> x a p s", a=2, s=2),
+                in_=bank_x[(pair, bs)][:].rearrange("x (a s p) -> x a p s", a=2, s=2),
+            )
 
         def q_x(pair, bs):
             if not ok(pair):
@@ -223,7 +222,7 @@ def tile_gcrnncell_pb_t_kernel(tc, r_prev, h_diff, u, state, support0, support1,
             if not ok(pair):
                 return
             if bs == 0:
-                cand[pair] = work.tile([P, 1024], F32, name="cand", tag="cand", bufs=3)
+                cand[pair] = work.tile([P, 1024], F32, name="cand", tag="cand")
             nc.scalar.activation(out=cand[pair][:, 512 * bs : 512 * bs + 512], in_=bank_o[(pair, bs)][:], func=TANH)
 
         def tr_s(pair):
@@ -237,36 +236,44 @@ def tile_gcrnncell_pb_t_kernel(tc, r_prev, h_diff, u, state, support0, support1,
                     nc.tensor.transpose(out=bank[:, 128 * g : 128 * g + 128], in_=view[:, b, :, s], identity=ident[:])
             bank_s[pair] = bank
 
-        def blend_d(pair):
+        def cuts(pair):
+            if pair == PAIRS - 1:
+                return ((0, 1), (1, 2))
+            return ((0, 2),)
+
+        def keep_part(pair):
             if not ok(pair):
                 return
             t = work.tile([P, 1024], F32, name="mix", tag="mix", bufs=4)
             nc.vector.tensor_tensor(
                 out=t[:].rearrange("p (g e k) -> p g e k", g=4, e=2),
                 in0=bank_s[pair][:].bitcast(BF16).rearrange("p (g k e) -> p g e k", g=4, e=2),
-                in1=cand[pair][:].rearrange("p (g e k) -> p g e k", g=4, e=2),
-                op=ALU.subtract,
+                in1=u_raw[pair][:].rearrange("p (g e k) -> p g e k", g=4, e=2),
+                op=ALU.mult,
             )
             mix[pair] = t
 
-        def blend_e(pair):
+        def new_part(pair):
             if not ok(pair):
                 return
-            t = mix[pair]
-            nc.vector.tensor_tensor(out=t[:], in0=t[:], in1=u_raw[pair][:], op=ALU.mult)
+            c = cand[pair]
+            for lo, hi in cuts(pair):
+                cols = slice(512 * lo, 512 * hi)
+                nc.vector.scalar_tensor_tensor(
+                    out=c[:, cols], in0=u_raw[pair][:, cols], scalar=1.0, in1=c[:, cols], op0=ALU.subtract, op1=ALU.mult
+                )
 
         def blend_z(pair):
             if not ok(pair):
                 return
             t = mix[pair]
-            if pair < PAIRS - POOL_TAIL:
-                nc.gpsimd.tensor_tensor(out=t[:], in0=t[:], in1=cand[pair][:], op=ALU.add)
-            else:
-                nc.vector.tensor_tensor(out=t[:], in0=t[:], in1=cand[pair][:], op=ALU.add)
-            nc.sync.dma_start(
-                out=out[2 * pair : 2 * pair + 2].rearrange("b (p f) -> p b f", p=P),
-                in_=t[:].rearrange("p (b f) -> p b f", b=2),
-            )
+            for lo, hi in cuts(pair):
+                cols = slice(512 * lo, 512 * hi)
+                nc.vector.tensor_tensor(out=t[:, cols], in0=t[:, cols], in1=cand[pair][:, cols], op=ALU.subtract)
+                nc.sync.dma_start(
+                    out=out[2 * pair + lo : 2 * pair + hi].rearrange("b (p f) -> p b f", p=P),
+                    in_=t[:, cols].rearrange("p (b f) -> p b f", f=512),
+                )
 
         ident = const.tile([P, P], F32, name="ident")
         make_identity(nc, ident[:])
@@ -279,8 +286,14 @@ def tile_gcrnncell_pb_t_kernel(tc, r_prev, h_diff, u, state, support0, support1,
         ck_h = c_kernel[0:256, :].rearrange("(q t) u -> q (t u)", t=4)
         ck_c = c_kernel[256:512, :].rearrange("(i q h) u -> q i (h u)", i=2, h=2)
 
+        def fetch(step):
+            load_r(step + RL)
+            load_h(step + XL)
+            load_s(step)
+            load_u(step)
+
         sup_raw = []
-        load_r(0)
+        fetch(-1)
         for i, sup in enumerate((support0, support1)):
             t = const.tile([P, 2048], BF16, name="sup_raw%d" % i)
             nc.sync.dma_start(out=t[:], in_=sup.rearrange("(p j) n -> p (j n)", j=4))
@@ -289,15 +302,8 @@ def tile_gcrnncell_pb_t_kernel(tc, r_prev, h_diff, u, state, support0, support1,
         nc.sync.dma_start(out=ck_raw[64:128, 512:1024], in_=ck_h)
         nc.sync.dma_start(out=ck_raw[0:64, 1024:1536].rearrange("q (i f) -> q i f", i=2), in_=ck_c)
         nc.sync.dma_start(out=ck_raw[64:128, 1536:2048].rearrange("q (i f) -> q i f", i=2), in_=ck_c)
-        for step in range(0, LOAD_BUFS + 3):
-            if 0 <= step < LOAD_BUFS:
-                load_h(step)
-            if 0 < step + 1 < LOAD_BUFS:
-                load_r(step + 1)
-            if 0 <= step - 2 < LOAD_BUFS:
-                load_s(step - 2)
-            if 0 <= step - 3 < LOAD_BUFS:
-                load_u(step - 3)
+        for step in range(0, FETCH - 1):
+            fetch(step)
 
         ck_grp = const.tile([P, 2048], BF16, name="ck_grp", align_bytes=64)
         ck_codes = const.tile([P, 512], U32, name="ck_codes", align_bytes=64)
@@ -335,41 +341,34 @@ def tile_gcrnncell_pb_t_kernel(tc, r_prev, h_diff, u, state, support0, support1,
                     in_=sup_grp[:, 2048 * a : 2048 * a + 2048],
                 )
 
-        for step in range(-1, PAIRS + 3):
+        for step in range(-1, PAIRS + 2):
             q_y(step - 1)
-            blend_e(step - 3)
-            blend_z(step - 3)
-            tr_r(step + 1)
-            tr_s(step - 2)
-            blend_d(step - 2)
-            ev_r(step + 1)
+            tr_r(step + RL)
+            ev_r(step + RL)
+            tr_x(step + XL, 0)
+            new_part(step - 2)
+            ev_x(step + XL, 0)
             mx1(step, 0)
             mx1(step, 1)
             mx2(step - 1, 0)
             ev_y(step, 0)
             ev_y(step, 1)
             tanh(step - 1, 0)
-            tr_x(step, 0)
-            tr_x(step, 1)
-            ev_x(step, 0)
-            ev_x(step, 1)
-            q_r(step + 1)
-            q_x(step, 0)
-            q_x(step, 1)
+            q_r(step + RL)
+            q_x(step + XL, 0)
+            blend_z(step - 2)
+            tr_x(step + XL, 1)
+            tr_s(step)
+            keep_part(step)
+            ev_x(step + XL, 1)
             mx1(step, 2)
             mx1(step, 3)
             mx2(step - 1, 1)
             ev_y(step, 2)
             ev_y(step, 3)
             tanh(step - 1, 1)
-            if step + 1 >= 0:
-                load_r(step + 1 + LOAD_BUFS)
-            if step >= 0:
-                load_h(step + LOAD_BUFS)
-            if step - 2 >= 0:
-                load_s(step - 2 + LOAD_BUFS)
-            if step - 3 >= 0:
-                load_u(step - 3 + LOAD_BUFS)
+            q_x(step + XL, 1)
+            fetch(step + FETCH)
             if step == -1:
                 prepare_supports()
                 prepare_kernel()

@@ -203,7 +203,7 @@ def tile_gcrnncell_pb_t_kernel(tc, r_prev, h_diff, u, state, support0, support1,
                     lhsT=xc[:, xcol : xcol + 128].bitcast(FP8X4),
                     lhsT_scale=xs[:, xcol : xcol + 128],
                     rhs=ck_codes[:, kx : kx + 128].bitcast(FP8X4),
-                    rhs_scale=ck_scales[:, kx : kx + 128],
+                    rhs_scale=ck_scales[:, 0:128],
                     start=True,
                     stop=False,
                 )
@@ -212,7 +212,7 @@ def tile_gcrnncell_pb_t_kernel(tc, r_prev, h_diff, u, state, support0, support1,
                     lhsT=yc[:, 128 * j : 128 * j + 128].bitcast(FP8X4),
                     lhsT_scale=ys[:, 128 * j : 128 * j + 128],
                     rhs=ck_codes[:, ky : ky + 128].bitcast(FP8X4),
-                    rhs_scale=ck_scales[:, ky : ky + 128],
+                    rhs_scale=ck_scales[:, 128:256],
                     start=False,
                     stop=True,
                 )
@@ -281,8 +281,9 @@ def tile_gcrnncell_pb_t_kernel(tc, r_prev, h_diff, u, state, support0, support1,
         nc.vector.memset(warm[:], 0.0)
         nc.scalar.activation(out=warm[:, 1:2], in_=warm[:, 0:1], func=TANH)
 
-        ck_raw = const.tile([P, 2048], BF16, name="ck_raw")
-        nc.vector.memset(ck_raw[:].bitcast(I32), 0)
+        ck_raw = const.tile([P, 1024], BF16, name="ck_raw")
+        ck_codes = const.tile([P, 512], U32, name="ck_codes", align_bytes=64)
+        nc.gpsimd.memset(ck_codes[:].bitcast(I32), 0)
         ck_h = c_kernel[0:256, :].rearrange("(q t) u -> q (t u)", t=4)
         ck_c = c_kernel[256:512, :].rearrange("(i q h) u -> q i (h u)", i=2, h=2)
 
@@ -299,25 +300,29 @@ def tile_gcrnncell_pb_t_kernel(tc, r_prev, h_diff, u, state, support0, support1,
             nc.sync.dma_start(out=t[:], in_=sup.rearrange("(p j) n -> p (j n)", j=4))
             sup_raw.append(t)
         nc.sync.dma_start(out=ck_raw[0:64, 0:512], in_=ck_h)
-        nc.sync.dma_start(out=ck_raw[64:128, 512:1024], in_=ck_h)
-        nc.sync.dma_start(out=ck_raw[0:64, 1024:1536].rearrange("q (i f) -> q i f", i=2), in_=ck_c)
-        nc.sync.dma_start(out=ck_raw[64:128, 1536:2048].rearrange("q (i f) -> q i f", i=2), in_=ck_c)
+        nc.sync.dma_start(out=ck_raw[64:128, 0:512], in_=ck_h)
+        nc.sync.dma_start(out=ck_raw[0:64, 512:1024].rearrange("q (i f) -> q i f", i=2), in_=ck_c)
+        nc.sync.dma_start(out=ck_raw[64:128, 512:1024].rearrange("q (i f) -> q i f", i=2), in_=ck_c)
         for step in range(0, FETCH - 1):
             fetch(step)
 
-        ck_grp = const.tile([P, 2048], BF16, name="ck_grp", align_bytes=64)
-        ck_codes = const.tile([P, 512], U32, name="ck_codes", align_bytes=64)
-        ck_scales = const.tile([P, 512], U8, name="ck_scales", align_bytes=64)
+        ck_grp = const.tile([P, 1024], BF16, name="ck_grp", align_bytes=64)
+        ck_both = const.tile([P, 256], U32, name="ck_both", align_bytes=64)
+        ck_scales = const.tile([P, 256], U8, name="ck_scales", align_bytes=64)
         sup_grp = const.tile([P, 4096], BF16, name="sup_grp", align_bytes=64)
         sup_codes = const.tile([P, 1024], U32, name="sup_codes", align_bytes=64)
         sup_scales = const.tile([P, 1024], U8, name="sup_scales", align_bytes=64)
 
         def prepare_kernel():
             nc.vector.tensor_copy(
-                out=ck_grp[:].rearrange("p (v u t) -> p v u t", v=4, t=4),
-                in_=ck_raw[:].rearrange("p (v t u) -> p v u t", v=4, t=4),
+                out=ck_grp[:].rearrange("p (v u t) -> p v u t", v=2, t=4),
+                in_=ck_raw[:].rearrange("p (v t u) -> p v u t", v=2, t=4),
             )
-            nc.vector.quantize_mx(out=ck_codes[:].bitcast(FP8X4), scales=ck_scales[:], in_=ck_grp[:])
+            nc.vector.quantize_mx(out=ck_both[:].bitcast(FP8X4), scales=ck_scales[:], in_=ck_grp[:])
+            dst = ck_codes[:].bitcast(I32).rearrange("p (v s u) -> p v s u", v=2, s=2)
+            codes = ck_both[:].bitcast(I32).rearrange("p (v u) -> p v u", v=2)
+            nc.vector.tensor_copy(out=dst[0:64, :, 0, :], in_=codes[0:64])
+            nc.vector.tensor_copy(out=dst[64:128, :, 1, :], in_=codes[64:128])
 
         def prepare_supports():
             grp_words = sup_grp[:].bitcast(F32).rearrange("w (a b i f) -> w a b i f", a=2, b=2, i=2)

@@ -15,6 +15,10 @@ ALU = mybir.AluOpType
 P = 128
 PAIRS = 16
 FETCH = 3
+GC = 384
+VR = ()
+VX = ()
+SL = 1
 MANUAL = True
 RL = 1
 XL = 0
@@ -94,7 +98,7 @@ def tile_gcrnncell_pb_t_kernel(tc, r_prev, h_diff, u, state, support0, support1,
         def tr_r(pair):
             if not ok(pair):
                 return
-            bank = psum.tile([P, 512], F32, name="bank_r", tag="bank_r", bufs=1)
+            bank = psum.tile([P, 512], F32, name="bank_r", tag="bank_x")
             words = r_raw[pair][:].bitcast(F32)
             for g in range(4):
                 nc.tensor.transpose(out=bank[:, 128 * g : 128 * g + 128], in_=words[:, 128 * g : 128 * g + 128], identity=ident[:])
@@ -104,7 +108,7 @@ def tile_gcrnncell_pb_t_kernel(tc, r_prev, h_diff, u, state, support0, support1,
             if not ok(pair):
                 return
             grp = work.tile([P, 1024], BF16, name="r_grp", tag="r_grp", align_bytes=64)
-            nc.scalar.copy(
+            (nc.vector.tensor_copy if pair in VR else nc.scalar.copy)(
                 out=grp[:].bitcast(F32).rearrange("w (h c t) -> w h c t", h=2, t=2),
                 in_=bank_r[pair][:].rearrange("w (h t c) -> w h c t", h=2, t=2),
             )
@@ -134,24 +138,18 @@ def tile_gcrnncell_pb_t_kernel(tc, r_prev, h_diff, u, state, support0, support1,
                 return
             if bs == 0:
                 x_grp[pair] = work.tile([P, 2048], BF16, name="x_grp", tag="x_grp", align_bytes=64)
-            nc.scalar.copy(
+            (nc.vector.tensor_copy if (pair, bs) in VX else nc.scalar.copy)(
                 out=x_grp[pair][:].bitcast(F32)[:, 512 * bs : 512 * bs + 512].rearrange("x (a p s) -> x a p s", a=2, s=2),
                 in_=bank_x[(pair, bs)][:].rearrange("x (a s p) -> x a p s", a=2, s=2),
             )
 
-        def q_x(pair, bs):
+        def q_x(pair):
             if not ok(pair):
                 return
-            if bs == 0:
-                codes = work.tile([P, 512], U32, name="x_codes", tag="x_codes", bufs=3, align_bytes=64)
-                scales = work.tile([P, 512], U8, name="x_scales", tag="x_scales", bufs=3, align_bytes=64)
-                x_mx[pair] = (codes, scales)
-            codes, scales = x_mx[pair]
-            nc.vector.quantize_mx(
-                out=codes[:, 256 * bs : 256 * bs + 256].bitcast(FP8X4),
-                scales=scales[:, 256 * bs : 256 * bs + 256],
-                in_=x_grp[pair][:, 1024 * bs : 1024 * bs + 1024],
-            )
+            codes = work.tile([P, 512], U32, name="x_codes", tag="x_codes", bufs=3, align_bytes=64)
+            scales = work.tile([P, 512], U8, name="x_scales", tag="x_scales", bufs=3, align_bytes=64)
+            x_mx[pair] = (codes, scales)
+            nc.vector.quantize_mx(out=codes[:].bitcast(FP8X4), scales=scales[:], in_=x_grp[pair][:])
 
         def mx1(pair, j):
             if not ok(pair):
@@ -180,13 +178,19 @@ def tile_gcrnncell_pb_t_kernel(tc, r_prev, h_diff, u, state, support0, support1,
                 in_=bank_y[(pair, j)][:].rearrange("c (h i p) -> c p i h", h=2, i=2),
             )
 
-        def q_y(pair):
+        def q_y(pair, lo=0, hi=4):
             if not ok(pair):
                 return
-            codes = work.tile([P, 512], U32, name="y_codes", tag="y_codes", align_bytes=64)
-            scales = work.tile([P, 512], U8, name="y_scales", tag="y_scales", align_bytes=64)
-            nc.vector.quantize_mx(out=codes[:].bitcast(FP8X4), scales=scales[:], in_=y_grp[pair][:])
-            y_mx[pair] = (codes, scales)
+            if lo == 0:
+                codes = work.tile([P, 512], U32, name="y_codes", tag="y_codes", align_bytes=64)
+                scales = work.tile([P, 512], U8, name="y_scales", tag="y_scales", align_bytes=64)
+                y_mx[pair] = (codes, scales)
+            codes, scales = y_mx[pair]
+            nc.vector.quantize_mx(
+                out=codes[:, 128 * lo : 128 * hi].bitcast(FP8X4),
+                scales=scales[:, 128 * lo : 128 * hi],
+                in_=y_grp[pair][:, 512 * lo : 512 * hi],
+            )
 
         def mx2(pair, bs):
             if not ok(pair):
@@ -222,13 +226,51 @@ def tile_gcrnncell_pb_t_kernel(tc, r_prev, h_diff, u, state, support0, support1,
             if not ok(pair):
                 return
             if bs == 0:
-                cand[pair] = work.tile([P, 1024], F32, name="cand", tag="cand")
+                cand[pair] = work.tile([P, 1024], F32, name="cand", tag="cand", bufs=3)
             nc.scalar.activation(out=cand[pair][:, 512 * bs : 512 * bs + 512], in_=bank_o[(pair, bs)][:], func=TANH)
+
+        def mx2_tail(pair, half):
+            bank = psum.tile([P, 512], F32, name="bank_o", tag="bank_o")
+            xc, xs = x_mx[pair]
+            yc, ys = y_mx[pair]
+            for b in range(2):
+                for i in range(2):
+                    j = 2 * half + i
+                    dst = bank[:, 256 * b + 128 * i : 256 * b + 128 * i + 128]
+                    xcol = 256 * b + 128 * half
+                    kx = 128 * i
+                    ky = 128 * (2 + b)
+                    nc.tensor.matmul_mx(
+                        out=dst,
+                        lhsT=xc[:, xcol : xcol + 128].bitcast(FP8X4),
+                        lhsT_scale=xs[:, xcol : xcol + 128],
+                        rhs=ck_codes[:, kx : kx + 128].bitcast(FP8X4),
+                        rhs_scale=ck_scales[:, 0:128],
+                        start=True,
+                        stop=False,
+                    )
+                    nc.tensor.matmul_mx(
+                        out=dst,
+                        lhsT=yc[:, 128 * j : 128 * j + 128].bitcast(FP8X4),
+                        lhsT_scale=ys[:, 128 * j : 128 * j + 128],
+                        rhs=ck_codes[:, ky : ky + 128].bitcast(FP8X4),
+                        rhs_scale=ck_scales[:, 128:256],
+                        start=False,
+                        stop=True,
+                    )
+            bank_o[(pair, half)] = bank
+
+        def tanh_tail(pair, half):
+            if half == 0:
+                cand[pair] = work.tile([P, 1024], F32, name="cand", tag="cand", bufs=3)
+            nc.scalar.activation(
+                out=cand[pair][:, 512 * half : 512 * half + 512].rearrange("p (b f) -> p b f", b=2), in_=bank_o[(pair, half)][:].rearrange("p (b f) -> p b f", b=2), func=TANH
+            )
 
         def tr_s(pair):
             if not ok(pair):
                 return
-            bank = psum.tile([P, 512], F32, name="bank_s", tag="bank_s", bufs=1)
+            bank = psum.tile([P, 512], F32, name="bank_s", tag="bank_s")
             view = s_raw[pair][:].bitcast(F32).rearrange("k (b x s) -> k b x s", b=2, s=2)
             for b in range(2):
                 for s in range(2):
@@ -236,44 +278,63 @@ def tile_gcrnncell_pb_t_kernel(tc, r_prev, h_diff, u, state, support0, support1,
                     nc.tensor.transpose(out=bank[:, 128 * g : 128 * g + 128], in_=view[:, b, :, s], identity=ident[:])
             bank_s[pair] = bank
 
-        def cuts(pair):
-            if pair == PAIRS - 1:
-                return ((0, 1), (1, 2))
-            return ((0, 2),)
-
         def keep_part(pair):
             if not ok(pair):
                 return
-            t = work.tile([P, 1024], F32, name="mix", tag="mix", bufs=4)
-            nc.vector.tensor_tensor(
-                out=t[:].rearrange("p (g e k) -> p g e k", g=4, e=2),
-                in0=bank_s[pair][:].bitcast(BF16).rearrange("p (g k e) -> p g e k", g=4, e=2),
-                in1=u_raw[pair][:].rearrange("p (g e k) -> p g e k", g=4, e=2),
-                op=ALU.mult,
-            )
+            t = work.tile([P, 1024], F32, name="mix", tag="mix", bufs=5)
+            prev = bank_s[pair][:].bitcast(BF16).rearrange("p (g k e) -> p g e k", g=4, e=2)
+            gate = u_raw[pair][:].rearrange("p (g e k) -> p g e k", g=4, e=2)
+            if pair < PAIRS - 1:
+                nc.vector.tensor_tensor(out=t[:].rearrange("p (g e k) -> p g e k", g=4, e=2), in0=prev, in1=gate, op=ALU.mult)
+            else:
+                dst = t[:].rearrange("p (s b e k) -> p s b e k", s=2, b=2, e=2)
+                for b in range(2):
+                    nc.vector.tensor_tensor(
+                        out=dst[:, :, b], in0=prev[:, 2 * b : 2 * b + 2], in1=gate[:, 2 * b : 2 * b + 2], op=ALU.mult
+                    )
             mix[pair] = t
 
-        def new_part(pair):
+        def new_part(pair, lo=0, hi=1024):
             if not ok(pair):
                 return
-            c = cand[pair]
-            for lo, hi in cuts(pair):
-                cols = slice(512 * lo, 512 * hi)
-                nc.vector.scalar_tensor_tensor(
-                    out=c[:, cols], in0=u_raw[pair][:, cols], scalar=1.0, in1=c[:, cols], op0=ALU.subtract, op1=ALU.mult
-                )
+            c = cand[pair][:, lo:hi]
+            nc.vector.scalar_tensor_tensor(out=c, in0=u_raw[pair][:, lo:hi], scalar=1.0, in1=c, op0=ALU.subtract, op1=ALU.mult)
+
+        def new_tail(pair, half):
+            c = cand[pair][:, 512 * half : 512 * half + 512].rearrange("p (b f) -> p b f", b=2)
+            u_half = u_raw[pair][:].rearrange("p (b f) -> p b f", b=2)[:, :, 256 * half : 256 * half + 256]
+            nc.vector.scalar_tensor_tensor(out=c, in0=u_half, scalar=1.0, in1=c, op0=ALU.subtract, op1=ALU.mult)
+
+        def blend_g(pair):
+            if not ok(pair) or pair >= PAIRS - 2:
+                return
+            t = mix[pair]
+            cols = slice(1024 - GC, 1024)
+            nc.gpsimd.tensor_tensor(out=t[:, cols], in0=t[:, cols], in1=cand[pair][:, cols], op=ALU.subtract)
+
+        def subtract(pair, lo, hi):
+            t = mix[pair]
+            nc.vector.tensor_tensor(out=t[:, lo:hi], in0=t[:, lo:hi], in1=cand[pair][:, lo:hi], op=ALU.subtract)
+
+        def store(pair):
+            return out[2 * pair : 2 * pair + 2].rearrange("b (p f) -> p b f", p=P)
 
         def blend_z(pair):
             if not ok(pair):
                 return
-            t = mix[pair]
-            for lo, hi in cuts(pair):
-                cols = slice(512 * lo, 512 * hi)
-                nc.vector.tensor_tensor(out=t[:, cols], in0=t[:, cols], in1=cand[pair][:, cols], op=ALU.subtract)
-                nc.sync.dma_start(
-                    out=out[2 * pair + lo : 2 * pair + hi].rearrange("b (p f) -> p b f", p=P),
-                    in_=t[:, cols].rearrange("p (b f) -> p b f", f=512),
-                )
+            subtract(pair, 0, 1024 - GC)
+            nc.sync.dma_start(out=store(pair), in_=mix[pair][:].rearrange("p (b f) -> p b f", f=512))
+
+        def blend_batch(pair, b):
+            subtract(pair, 512 * b, 512 * b + 512)
+            nc.sync.dma_start(out=store(pair)[:, b, :], in_=mix[pair][:, 512 * b : 512 * b + 512])
+
+        def blend_tail(pair, half):
+            subtract(pair, 512 * half, 512 * half + 512)
+            nc.sync.dma_start(
+                out=store(pair)[:, :, 256 * half : 256 * half + 256],
+                in_=mix[pair][:, 512 * half : 512 * half + 512].rearrange("p (b f) -> p b f", b=2),
+            )
 
         ident = const.tile([P, P], F32, name="ident")
         make_identity(nc, ident[:])
@@ -287,23 +348,41 @@ def tile_gcrnncell_pb_t_kernel(tc, r_prev, h_diff, u, state, support0, support1,
         ck_h = c_kernel[0:256, :].rearrange("(q t) u -> q (t u)", t=4)
         ck_c = c_kernel[256:512, :].rearrange("(i q h) u -> q i (h u)", i=2, h=2)
 
-        def fetch(step):
-            load_r(step + RL)
-            load_h(step + XL)
-            load_s(step)
-            load_u(step)
+        def load_ck():
+            nc.sync.dma_start(out=ck_raw[0:64, 0:512], in_=ck_h)
+            nc.sync.dma_start(out=ck_raw[64:128, 0:512], in_=ck_h)
+            nc.sync.dma_start(out=ck_raw[0:64, 512:1024].rearrange("q (i f) -> q i f", i=2), in_=ck_c)
+            nc.sync.dma_start(out=ck_raw[64:128, 512:1024].rearrange("q (i f) -> q i f", i=2), in_=ck_c)
 
         sup_raw = []
-        fetch(-1)
-        for i, sup in enumerate((support0, support1)):
+        load_r(0)
+        for i in range(2):
             t = const.tile([P, 2048], BF16, name="sup_raw%d" % i)
-            nc.sync.dma_start(out=t[:], in_=sup.rearrange("(p j) n -> p (j n)", j=4))
             sup_raw.append(t)
-        nc.sync.dma_start(out=ck_raw[0:64, 0:512], in_=ck_h)
-        nc.sync.dma_start(out=ck_raw[64:128, 0:512], in_=ck_h)
-        nc.sync.dma_start(out=ck_raw[0:64, 512:1024].rearrange("q (i f) -> q i f", i=2), in_=ck_c)
-        nc.sync.dma_start(out=ck_raw[64:128, 512:1024].rearrange("q (i f) -> q i f", i=2), in_=ck_c)
-        for step in range(0, FETCH - 1):
+        for a in range(2):
+            for t, sup in zip(sup_raw, (support0, support1)):
+                nc.sync.dma_start(
+                    out=t[:, 1024 * a : 1024 * a + 1024],
+                    in_=sup.rearrange("(p a j) n -> p a (j n)", a=2, j=2)[:, a, :],
+                )
+        load_r(1)
+        load_ck()
+        load_h(0)
+        load_s(0)
+        load_u(0)
+        load_r(2)
+        load_h(1)
+        load_s(1)
+        load_s(2)
+        load_u(1)
+
+        def fetch(step):
+            load_r(step + 1)
+            load_h(step)
+            load_s(step + 1)
+            load_u(step)
+
+        for step in range(2, FETCH):
             fetch(step)
 
         ck_grp = const.tile([P, 1024], BF16, name="ck_grp", align_bytes=64)
@@ -324,56 +403,103 @@ def tile_gcrnncell_pb_t_kernel(tc, r_prev, h_diff, u, state, support0, support1,
             nc.vector.tensor_copy(out=dst[0:64, :, 0, :], in_=codes[0:64])
             nc.vector.tensor_copy(out=dst[64:128, :, 1, :], in_=codes[64:128])
 
-        def prepare_supports():
-            grp_words = sup_grp[:].bitcast(F32).rearrange("w (a b i f) -> w a b i f", a=2, b=2, i=2)
+        grp_words = sup_grp[:].bitcast(F32).rearrange("w (a b i f) -> w a b i f", a=2, b=2, i=2)
+
+        def prepare_supports(a):
             for i in range(2):
                 words = sup_raw[i][:].bitcast(F32)
-                for a in range(2):
-                    bank = psum.tile([P, 512], F32, name="bank_c", tag=("bank_x" if i == 0 else "bank_y"))
-                    for g in range(4):
-                        col = 512 * a + 128 * g
-                        nc.tensor.transpose(out=bank[:, 128 * g : 128 * g + 128], in_=words[:, col : col + 128], identity=ident[:])
-                    dst = grp_words[:, a, :, i, :].rearrange("w b (p t) -> w b p t", t=2)
-                    src = bank[:].rearrange("w (b t p) -> w b p t", b=2, t=2)
-                    if a == 0:
-                        nc.vector.tensor_copy(out=dst, in_=src)
-                    else:
-                        nc.scalar.copy(out=dst, in_=src)
-            for a in range(2):
-                nc.vector.quantize_mx(
-                    out=sup_codes[:, 512 * a : 512 * a + 512].bitcast(FP8X4),
-                    scales=sup_scales[:, 512 * a : 512 * a + 512],
-                    in_=sup_grp[:, 2048 * a : 2048 * a + 2048],
-                )
+                bank = psum.tile([P, 512], F32, name="bank_c", tag=("bank_x" if i == 0 else "bank_y"))
+                for g in range(4):
+                    col = 512 * a + 128 * g
+                    nc.tensor.transpose(out=bank[:, 128 * g : 128 * g + 128], in_=words[:, col : col + 128], identity=ident[:])
+                dst = grp_words[:, a, :, i, :].rearrange("w b (p t) -> w b p t", t=2)
+                src = bank[:].rearrange("w (b t p) -> w b p t", b=2, t=2)
+                if i == 0:
+                    nc.vector.tensor_copy(out=dst, in_=src)
+                else:
+                    nc.scalar.copy(out=dst, in_=src)
 
-        for step in range(-1, PAIRS + 2):
+        def quantise_supports(a):
+            nc.vector.quantize_mx(
+                out=sup_codes[:, 512 * a : 512 * a + 512].bitcast(FP8X4),
+                scales=sup_scales[:, 512 * a : 512 * a + 512],
+                in_=sup_grp[:, 2048 * a : 2048 * a + 2048],
+            )
+
+        tr_r(0)
+        ev_r(0)
+        q_r(0)
+        prepare_supports(0)
+        prepare_supports(1)
+        quantise_supports(0)
+        tr_r(1)
+        ev_r(1)
+        quantise_supports(1)
+        q_r(1)
+        mx1(0, 0)
+        mx1(0, 1)
+        ev_y(0, 0)
+        ev_y(0, 1)
+        prepare_kernel()
+        tr_x(0, 0)
+        tr_x(0, 1)
+        ev_x(0, 0)
+        ev_x(0, 1)
+        q_x(0)
+        tr_s(0)
+        keep_part(0)
+        mx1(0, 2)
+        mx1(0, 3)
+        ev_y(0, 2)
+        ev_y(0, 3)
+        fetch(FETCH)
+        for step in range(1, PAIRS):
+            last = step == PAIRS - 1
             q_y(step - 1)
-            tr_r(step + RL)
-            ev_r(step + RL)
-            tr_x(step + XL, 0)
-            new_part(step - 2)
-            ev_x(step + XL, 0)
+            tr_r(step + 1)
+            ev_r(step + 1)
+            tr_x(step, 0)
+            ev_x(step, 0)
+            if step == 1:
+                tr_s(1)
             mx1(step, 0)
             mx1(step, 1)
             mx2(step - 1, 0)
             ev_y(step, 0)
             ev_y(step, 1)
             tanh(step - 1, 0)
-            q_r(step + RL)
-            q_x(step + XL, 0)
-            blend_z(step - 2)
-            tr_x(step + XL, 1)
-            tr_s(step)
+            new_part(step - 2)
+            q_r(step + 1)
+            blend_g(step - 2)
+            tr_x(step, 1)
+            tr_s(step + 1)
             keep_part(step)
-            ev_x(step + XL, 1)
+            if not last:
+                blend_z(step - 2)
+            ev_x(step, 1)
             mx1(step, 2)
             mx1(step, 3)
             mx2(step - 1, 1)
             ev_y(step, 2)
             ev_y(step, 3)
             tanh(step - 1, 1)
-            q_x(step + XL, 1)
+            if not last:
+                q_x(step)
             fetch(step + FETCH)
-            if step == -1:
-                prepare_supports()
-                prepare_kernel()
+        a, b = PAIRS - 2, PAIRS - 1
+        q_x(b)
+        q_y(b, 0, 2)
+        new_part(a, 0, 512)
+        mx2_tail(b, 0)
+        tanh_tail(b, 0)
+        q_y(b, 2, 4)
+        blend_z(a - 1)
+        blend_batch(a, 0)
+        new_part(a, 512, 1024)
+        mx2_tail(b, 1)
+        tanh_tail(b, 1)
+        new_tail(b, 0)
+        blend_batch(a, 1)
+        blend_tail(b, 0)
+        new_tail(b, 1)
+        blend_tail(b, 1)

@@ -15,9 +15,7 @@ ALU = mybir.AluOpType
 P = 128
 PAIRS = 16
 FETCH = 3
-GC = 384
-VR = ()
-VX = ()
+GC = 448
 SL = 1
 MANUAL = True
 RL = 1
@@ -108,7 +106,7 @@ def tile_gcrnncell_pb_t_kernel(tc, r_prev, h_diff, u, state, support0, support1,
             if not ok(pair):
                 return
             grp = work.tile([P, 1024], BF16, name="r_grp", tag="r_grp", align_bytes=64)
-            (nc.vector.tensor_copy if pair in VR else nc.scalar.copy)(
+            (nc.vector.tensor_copy if pair % 3 == 0 else nc.scalar.copy)(
                 out=grp[:].bitcast(F32).rearrange("w (h c t) -> w h c t", h=2, t=2),
                 in_=bank_r[pair][:].rearrange("w (h t c) -> w h c t", h=2, t=2),
             )
@@ -138,7 +136,7 @@ def tile_gcrnncell_pb_t_kernel(tc, r_prev, h_diff, u, state, support0, support1,
                 return
             if bs == 0:
                 x_grp[pair] = work.tile([P, 2048], BF16, name="x_grp", tag="x_grp", align_bytes=64)
-            (nc.vector.tensor_copy if (pair, bs) in VX else nc.scalar.copy)(
+            nc.scalar.copy(
                 out=x_grp[pair][:].bitcast(F32)[:, 512 * bs : 512 * bs + 512].rearrange("x (a p s) -> x a p s", a=2, s=2),
                 in_=bank_x[(pair, bs)][:].rearrange("x (a s p) -> x a p s", a=2, s=2),
             )

@@ -15,7 +15,6 @@ ALU = mybir.AluOpType
 P = 128
 PAIRS = 16
 FETCH = 3
-GC = 448
 SL = 1
 MANUAL = True
 RL = 1
@@ -106,7 +105,7 @@ def tile_gcrnncell_pb_t_kernel(tc, r_prev, h_diff, u, state, support0, support1,
             if not ok(pair):
                 return
             grp = work.tile([P, 1024], BF16, name="r_grp", tag="r_grp", align_bytes=64)
-            (nc.vector.tensor_copy if pair % 3 == 0 else nc.scalar.copy)(
+            nc.scalar.copy(
                 out=grp[:].bitcast(F32).rearrange("w (h c t) -> w h c t", h=2, t=2),
                 in_=bank_r[pair][:].rearrange("w (h t c) -> w h c t", h=2, t=2),
             )
@@ -131,12 +130,18 @@ def tile_gcrnncell_pb_t_kernel(tc, r_prev, h_diff, u, state, support0, support1,
                     nc.tensor.transpose(out=bank[:, 128 * g : 128 * g + 128], in_=view[:, bs, a, :, s], identity=ident[:])
             bank_x[(pair, bs)] = bank
 
+        def helped(pair):
+            return pair % 2 == 0 and 0 < pair < PAIRS - 1
+
+        def columns(pair):
+            return 576 if helped(pair + 2) else 384
+
         def ev_x(pair, bs):
             if not ok(pair):
                 return
             if bs == 0:
                 x_grp[pair] = work.tile([P, 2048], BF16, name="x_grp", tag="x_grp", align_bytes=64)
-            nc.scalar.copy(
+            (nc.vector.tensor_copy if bs == 1 and helped(pair) else nc.scalar.copy)(
                 out=x_grp[pair][:].bitcast(F32)[:, 512 * bs : 512 * bs + 512].rearrange("x (a p s) -> x a p s", a=2, s=2),
                 in_=bank_x[(pair, bs)][:].rearrange("x (a s p) -> x a p s", a=2, s=2),
             )
@@ -196,28 +201,29 @@ def tile_gcrnncell_pb_t_kernel(tc, r_prev, h_diff, u, state, support0, support1,
             bank = psum.tile([P, 512], F32, name="bank_o", tag="bank_o")
             xc, xs = x_mx[pair]
             yc, ys = y_mx[pair]
-            for j in range(4):
-                xcol = 256 * bs + 128 * (j // 2)
-                kx = 128 * (j % 2)
-                ky = 128 * (2 + bs)
+            ky = 128 * (2 + bs)
+            for a in range(2):
+                xcol = 256 * bs + 128 * a
                 nc.tensor.matmul_mx(
-                    out=bank[:, 128 * j : 128 * j + 128],
+                    out=bank[:, 256 * a : 256 * a + 256],
                     lhsT=xc[:, xcol : xcol + 128].bitcast(FP8X4),
                     lhsT_scale=xs[:, xcol : xcol + 128],
-                    rhs=ck_codes[:, kx : kx + 128].bitcast(FP8X4),
-                    rhs_scale=ck_scales[:, 0:128],
+                    rhs=ck_codes[:, 0:256].bitcast(FP8X4),
+                    rhs_scale=ck_scales[:, 0:256],
                     start=True,
                     stop=False,
                 )
-                nc.tensor.matmul_mx(
-                    out=bank[:, 128 * j : 128 * j + 128],
-                    lhsT=yc[:, 128 * j : 128 * j + 128].bitcast(FP8X4),
-                    lhsT_scale=ys[:, 128 * j : 128 * j + 128],
-                    rhs=ck_codes[:, ky : ky + 128].bitcast(FP8X4),
-                    rhs_scale=ck_scales[:, 128:256],
-                    start=False,
-                    stop=True,
-                )
+                for i in range(2):
+                    j = 2 * a + i
+                    nc.tensor.matmul_mx(
+                        out=bank[:, 128 * j : 128 * j + 128],
+                        lhsT=yc[:, 128 * j : 128 * j + 128].bitcast(FP8X4),
+                        lhsT_scale=ys[:, 128 * j : 128 * j + 128],
+                        rhs=ck_codes[:, ky : ky + 128].bitcast(FP8X4),
+                        rhs_scale=ck_scales[:, 256:384],
+                        start=False,
+                        stop=i == 1,
+                    )
             bank_o[(pair, bs)] = bank
 
         def tanh(pair, bs):
@@ -252,7 +258,7 @@ def tile_gcrnncell_pb_t_kernel(tc, r_prev, h_diff, u, state, support0, support1,
                         lhsT=yc[:, 128 * j : 128 * j + 128].bitcast(FP8X4),
                         lhsT_scale=ys[:, 128 * j : 128 * j + 128],
                         rhs=ck_codes[:, ky : ky + 128].bitcast(FP8X4),
-                        rhs_scale=ck_scales[:, 128:256],
+                        rhs_scale=ck_scales[:, 256:384],
                         start=False,
                         stop=True,
                     )
@@ -285,10 +291,14 @@ def tile_gcrnncell_pb_t_kernel(tc, r_prev, h_diff, u, state, support0, support1,
             if pair < PAIRS - 1:
                 nc.vector.tensor_tensor(out=t[:].rearrange("p (g e k) -> p g e k", g=4, e=2), in0=prev, in1=gate, op=ALU.mult)
             else:
-                dst = t[:].rearrange("p (s b e k) -> p s b e k", s=2, b=2, e=2)
-                for b in range(2):
+                prev = bank_s[pair][:].bitcast(BF16).rearrange("p (b s k e) -> p s b e k", b=2, s=2, e=2)
+                gate = u_raw[pair][:].rearrange("p (b s e k) -> p s b e k", b=2, s=2, e=2)
+                for s in range(2):
                     nc.vector.tensor_tensor(
-                        out=dst[:, :, b], in0=prev[:, 2 * b : 2 * b + 2], in1=gate[:, 2 * b : 2 * b + 2], op=ALU.mult
+                        out=t[:, 512 * s : 512 * s + 512].rearrange("p (b e k) -> p b e k", b=2, e=2),
+                        in0=prev[:, s],
+                        in1=gate[:, s],
+                        op=ALU.mult,
                     )
             mix[pair] = t
 
@@ -307,7 +317,7 @@ def tile_gcrnncell_pb_t_kernel(tc, r_prev, h_diff, u, state, support0, support1,
             if not ok(pair) or pair >= PAIRS - 2:
                 return
             t = mix[pair]
-            cols = slice(1024 - GC, 1024)
+            cols = slice(1024 - columns(pair), 1024)
             nc.gpsimd.tensor_tensor(out=t[:, cols], in0=t[:, cols], in1=cand[pair][:, cols], op=ALU.subtract)
 
         def subtract(pair, lo, hi):
@@ -320,7 +330,7 @@ def tile_gcrnncell_pb_t_kernel(tc, r_prev, h_diff, u, state, support0, support1,
         def blend_z(pair):
             if not ok(pair):
                 return
-            subtract(pair, 0, 1024 - GC)
+            subtract(pair, 0, 1024 - columns(pair))
             nc.sync.dma_start(out=store(pair), in_=mix[pair][:].rearrange("p (b f) -> p b f", f=512))
 
         def blend_batch(pair, b):
@@ -384,8 +394,8 @@ def tile_gcrnncell_pb_t_kernel(tc, r_prev, h_diff, u, state, support0, support1,
             fetch(step)
 
         ck_grp = const.tile([P, 1024], BF16, name="ck_grp", align_bytes=64)
-        ck_both = const.tile([P, 256], U32, name="ck_both", align_bytes=64)
-        ck_scales = const.tile([P, 256], U8, name="ck_scales", align_bytes=64)
+        ck_both = const.tile([P, 384], U32, name="ck_both", align_bytes=64)
+        ck_scales = const.tile([P, 384], U8, name="ck_scales", align_bytes=64)
         sup_grp = const.tile([P, 4096], BF16, name="sup_grp", align_bytes=64)
         sup_codes = const.tile([P, 1024], U32, name="sup_codes", align_bytes=64)
         sup_scales = const.tile([P, 1024], U8, name="sup_scales", align_bytes=64)
@@ -395,9 +405,14 @@ def tile_gcrnncell_pb_t_kernel(tc, r_prev, h_diff, u, state, support0, support1,
                 out=ck_grp[:].rearrange("p (v u t) -> p v u t", v=2, t=4),
                 in_=ck_raw[:].rearrange("p (v t u) -> p v u t", v=2, t=4),
             )
-            nc.vector.quantize_mx(out=ck_both[:].bitcast(FP8X4), scales=ck_scales[:], in_=ck_grp[:])
+            for v, lo in ((0, 0), (0, 128), (1, 256)):
+                nc.vector.quantize_mx(
+                    out=ck_both[:, lo : lo + 128].bitcast(FP8X4),
+                    scales=ck_scales[:, lo : lo + 128],
+                    in_=ck_grp[:, 512 * v : 512 * v + 512],
+                )
             dst = ck_codes[:].bitcast(I32).rearrange("p (v s u) -> p v s u", v=2, s=2)
-            codes = ck_both[:].bitcast(I32).rearrange("p (v u) -> p v u", v=2)
+            codes = ck_both[:, 128:384].bitcast(I32).rearrange("p (v u) -> p v u", v=2)
             nc.vector.tensor_copy(out=dst[0:64, :, 0, :], in_=codes[0:64])
             nc.vector.tensor_copy(out=dst[64:128, :, 1, :], in_=codes[64:128])
 
@@ -472,9 +487,12 @@ def tile_gcrnncell_pb_t_kernel(tc, r_prev, h_diff, u, state, support0, support1,
             tr_x(step, 1)
             tr_s(step + 1)
             keep_part(step)
+            if helped(step):
+                ev_x(step, 1)
             if not last:
                 blend_z(step - 2)
-            ev_x(step, 1)
+            if not helped(step):
+                ev_x(step, 1)
             mx1(step, 2)
             mx1(step, 3)
             mx2(step - 1, 1)
@@ -497,7 +515,7 @@ def tile_gcrnncell_pb_t_kernel(tc, r_prev, h_diff, u, state, support0, support1,
         mx2_tail(b, 1)
         tanh_tail(b, 1)
         new_tail(b, 0)
+        new_tail(b, 1)
         blend_batch(a, 1)
         blend_tail(b, 0)
-        new_tail(b, 1)
         blend_tail(b, 1)

@@ -134,7 +134,7 @@ def tile_gcrnncell_pb_t_kernel(tc, r_prev, h_diff, u, state, support0, support1,
             return pair % 2 == 0 and 0 < pair < PAIRS - 1
 
         def columns(pair):
-            return 576 if helped(pair + 2) else 384
+            return 704 if helped(pair + 2) else 448
 
         def ev_x(pair, bs):
             if not ok(pair):

from contextlib import ExitStack

import concourse.mybir as mybir
from concourse.masks import make_identity

F32 = mybir.dt.float32
BF16 = mybir.dt.bfloat16
U32 = mybir.dt.uint32
U8 = mybir.dt.uint8
I32 = mybir.dt.int32
FP8X4 = mybir.dt.float8_e4m3fn_x4
TANH = mybir.ActivationFunctionType.Tanh
ALU = mybir.AluOpType

P = 128
PAIRS = 16
FETCH = 3
SL = 1
MANUAL = True
RL = 1
XL = 0

FLOPS = 2 * 32 * 256 * 512 * 512 + 2 * 32 * 512 * 512 * 128


def tile_gcrnncell_pb_t_kernel(tc, r_prev, h_diff, u, state, support0, support1, c_kernel, out):
    nc = tc.nc
    r_rows = r_prev.rearrange("b k n -> (b k) n")
    with ExitStack() as ctx:
        const = ctx.enter_context(tc.tile_pool(name="const", bufs=1))
        loads = ctx.enter_context(tc.tile_pool(name="loads", bufs=FETCH + 2))
        work = ctx.enter_context(tc.tile_pool(name="work", bufs=2))
        psum = ctx.enter_context(tc.psum_pool(name="psum", bufs=2))
        if MANUAL:
            ctx.enter_context(tc.manual_schedule())

        r_raw = {}
        h_raw = {}
        s_raw = {}
        u_raw = {}
        bank_r = {}
        bank_x = {}
        bank_s = {}
        bank_y = {}
        bank_o = {}
        r_grp = {}
        r_mx = {}
        x_grp = {}
        x_mx = {}
        y_grp = {}
        y_mx = {}
        cand = {}
        mix = {}

        def ok(pair):
            return 0 <= pair < PAIRS

        def load_r(pair):
            if not ok(pair):
                return
            t = loads.tile([P, 1024], BF16, name="r_raw", tag="r_raw")
            nc.sync.dma_start(out=t[:], in_=r_rows[256 * pair : 256 * pair + 256, :].rearrange("(c h) n -> c (h n)", h=2))
            r_raw[pair] = t

        def load_h(pair):
            if not ok(pair):
                return
            t = loads.tile([P, 2048], BF16, name="h_raw", tag="h_raw")
            nc.sync.dma_start(
                out=t[:].rearrange("p (b f) -> p b f", b=2),
                in_=h_diff[2 * pair : 2 * pair + 2].rearrange("b (p j) c -> p b (j c)", j=4),
            )
            h_raw[pair] = t

        def load_s(pair):
            if not ok(pair):
                return
            t = loads.tile([P, 1024], BF16, name="s_raw", tag="s_raw")
            nc.sync.dma_start(
                out=t[:].rearrange("k (b n) -> k b n", b=2),
                in_=state[2 * pair : 2 * pair + 2].rearrange("b (k n) -> k b n", n=512),
            )
            s_raw[pair] = t

        def load_u(pair):
            if not ok(pair):
                return
            t = loads.tile([P, 1024], BF16, name="u_raw", tag="u_raw", bufs=FETCH + 4)
            nc.sync.dma_start(
                out=t[:].rearrange("p (b f) -> p b f", b=2),
                in_=u[2 * pair : 2 * pair + 2].rearrange("b (p j) k -> p b (j k)", j=4),
            )
            u_raw[pair] = t

        def tr_r(pair):
            if not ok(pair):
                return
            bank = psum.tile([P, 512], F32, name="bank_r", tag="bank_x")
            words = r_raw[pair][:].bitcast(F32)
            for g in range(4):
                nc.tensor.transpose(out=bank[:, 128 * g : 128 * g + 128], in_=words[:, 128 * g : 128 * g + 128], identity=ident[:])
            bank_r[pair] = bank

        def ev_r(pair):
            if not ok(pair):
                return
            grp = work.tile([P, 1024], BF16, name="r_grp", tag="r_grp", align_bytes=64)
            nc.scalar.copy(
                out=grp[:].bitcast(F32).rearrange("w (h c t) -> w h c t", h=2, t=2),
                in_=bank_r[pair][:].rearrange("w (h t c) -> w h c t", h=2, t=2),
            )
            r_grp[pair] = grp

        def q_r(pair):
            if not ok(pair):
                return
            codes = work.tile([P, 256], U32, name="r_codes", tag="r_codes", bufs=3, align_bytes=64)
            scales = work.tile([P, 256], U8, name="r_scales", tag="r_scales", bufs=3, align_bytes=64)
            nc.vector.quantize_mx(out=codes[:].bitcast(FP8X4), scales=scales[:], in_=r_grp[pair][:])
            r_mx[pair] = (codes, scales)

        def tr_x(pair, bs):
            if not ok(pair):
                return
            bank = psum.tile([P, 512], F32, name="bank_x", tag="bank_x")
            view = h_raw[pair][:].bitcast(F32).rearrange("p (b a x s) -> p b a x s", b=2, a=2, s=2)
            for a in range(2):
                for s in range(2):
                    g = 2 * a + s
                    nc.tensor.transpose(out=bank[:, 128 * g : 128 * g + 128], in_=view[:, bs, a, :, s], identity=ident[:])
            bank_x[(pair, bs)] = bank

        def helped(pair):
            return pair % 2 == 0 and 0 < pair < PAIRS - 1

        def columns(pair):
            return 704 if helped(pair + 2) else 448

        def ev_x(pair, bs):
            if not ok(pair):
                return
            if bs == 0:
                x_grp[pair] = work.tile([P, 2048], BF16, name="x_grp", tag="x_grp", align_bytes=64)
            (nc.vector.tensor_copy if bs == 1 and helped(pair) else nc.scalar.copy)(
                out=x_grp[pair][:].bitcast(F32)[:, 512 * bs : 512 * bs + 512].rearrange("x (a p s) -> x a p s", a=2, s=2),
                in_=bank_x[(pair, bs)][:].rearrange("x (a s p) -> x a p s", a=2, s=2),
            )

        def q_x(pair):
            if not ok(pair):
                return
            codes = work.tile([P, 512], U32, name="x_codes", tag="x_codes", bufs=3, align_bytes=64)
            scales = work.tile([P, 512], U8, name="x_scales", tag="x_scales", bufs=3, align_bytes=64)
            x_mx[pair] = (codes, scales)
            nc.vector.quantize_mx(out=codes[:].bitcast(FP8X4), scales=scales[:], in_=x_grp[pair][:])

        def mx1(pair, j):
            if not ok(pair):
                return
            bank = psum.tile([P, 512], F32, name="bank_y", tag="bank_y")
            codes, scales = r_mx[pair]
            for h in range(2):
                nc.tensor.matmul_mx(
                    out=bank[:, 256 * h : 256 * h + 256],
                    lhsT=codes[:, 128 * h : 128 * h + 128].bitcast(FP8X4),
                    lhsT_scale=scales[:, 128 * h : 128 * h + 128],
                    rhs=sup_codes[:, 256 * j : 256 * j + 256].bitcast(FP8X4),
                    rhs_scale=sup_scales[:, 256 * j : 256 * j + 256],
                    start=True,
                    stop=True,
                )
            bank_y[(pair, j)] = bank

        def ev_y(pair, j):
            if not ok(pair):
                return
            if j == 0:
                y_grp[pair] = work.tile([P, 2048], BF16, name="y_grp", tag="y_grp", align_bytes=64)
            nc.scalar.copy(
                out=y_grp[pair][:, 512 * j : 512 * j + 512].rearrange("c (p i h) -> c p i h", i=2, h=2),
                in_=bank_y[(pair, j)][:].rearrange("c (h i p) -> c p i h", h=2, i=2),
            )

        def q_y(pair, lo=0, hi=4):
            if not ok(pair):
                return
            if lo == 0:
                codes = work.tile([P, 512], U32, name="y_codes", tag="y_codes", align_bytes=64)
                scales = work.tile([P, 512], U8, name="y_scales", tag="y_scales", align_bytes=64)
                y_mx[pair] = (codes, scales)
            codes, scales = y_mx[pair]
            nc.vector.quantize_mx(
                out=codes[:, 128 * lo : 128 * hi].bitcast(FP8X4),
                scales=scales[:, 128 * lo : 128 * hi],
                in_=y_grp[pair][:, 512 * lo : 512 * hi],
            )

        def mx2(pair, bs):
            if not ok(pair):
                return
            bank = psum.tile([P, 512], F32, name="bank_o", tag="bank_o")
            xc, xs = x_mx[pair]
            yc, ys = y_mx[pair]
            ky = 128 * (2 + bs)
            for a in range(2):
                xcol = 256 * bs + 128 * a
                nc.tensor.matmul_mx(
                    out=bank[:, 256 * a : 256 * a + 256],
                    lhsT=xc[:, xcol : xcol + 128].bitcast(FP8X4),
                    lhsT_scale=xs[:, xcol : xcol + 128],
                    rhs=ck_codes[:, 0:256].bitcast(FP8X4),
                    rhs_scale=ck_scales[:, 0:256],
                    start=True,
                    stop=False,
                )
                for i in range(2):
                    j = 2 * a + i
                    nc.tensor.matmul_mx(
                        out=bank[:, 128 * j : 128 * j + 128],
                        lhsT=yc[:, 128 * j : 128 * j + 128].bitcast(FP8X4),
                        lhsT_scale=ys[:, 128 * j : 128 * j + 128],
                        rhs=ck_codes[:, ky : ky + 128].bitcast(FP8X4),
                        rhs_scale=ck_scales[:, 256:384],
                        start=False,
                        stop=i == 1,
                    )
            bank_o[(pair, bs)] = bank

        def tanh(pair, bs):
            if not ok(pair):
                return
            if bs == 0:
                cand[pair] = work.tile([P, 1024], F32, name="cand", tag="cand", bufs=3)
            nc.scalar.activation(out=cand[pair][:, 512 * bs : 512 * bs + 512], in_=bank_o[(pair, bs)][:], func=TANH)

        def mx2_tail(pair, half):
            bank = psum.tile([P, 512], F32, name="bank_o", tag="bank_o")
            xc, xs = x_mx[pair]
            yc, ys = y_mx[pair]
            for b in range(2):
                for i in range(2):
                    j = 2 * half + i
                    dst = bank[:, 256 * b + 128 * i : 256 * b + 128 * i + 128]
                    xcol = 256 * b + 128 * half
                    kx = 128 * i
                    ky = 128 * (2 + b)
                    nc.tensor.matmul_mx(
                        out=dst,
                        lhsT=xc[:, xcol : xcol + 128].bitcast(FP8X4),
                        lhsT_scale=xs[:, xcol : xcol + 128],
                        rhs=ck_codes[:, kx : kx + 128].bitcast(FP8X4),
                        rhs_scale=ck_scales[:, 0:128],
                        start=True,
                        stop=False,
                    )
                    nc.tensor.matmul_mx(
                        out=dst,
                        lhsT=yc[:, 128 * j : 128 * j + 128].bitcast(FP8X4),
                        lhsT_scale=ys[:, 128 * j : 128 * j + 128],
                        rhs=ck_codes[:, ky : ky + 128].bitcast(FP8X4),
                        rhs_scale=ck_scales[:, 256:384],
                        start=False,
                        stop=True,
                    )
            bank_o[(pair, half)] = bank

        def tanh_tail(pair, half):
            if half == 0:
                cand[pair] = work.tile([P, 1024], F32, name="cand", tag="cand", bufs=3)
            nc.scalar.activation(
                out=cand[pair][:, 512 * half : 512 * half + 512].rearrange("p (b f) -> p b f", b=2), in_=bank_o[(pair, half)][:].rearrange("p (b f) -> p b f", b=2), func=TANH
            )

        def tr_s(pair):
            if not ok(pair):
                return
            bank = psum.tile([P, 512], F32, name="bank_s", tag="bank_s")
            view = s_raw[pair][:].bitcast(F32).rearrange("k (b x s) -> k b x s", b=2, s=2)
            for b in range(2):
                for s in range(2):
                    g = 2 * b + s
                    nc.tensor.transpose(out=bank[:, 128 * g : 128 * g + 128], in_=view[:, b, :, s], identity=ident[:])
            bank_s[pair] = bank

        def keep_part(pair):
            if not ok(pair):
                return
            t = work.tile([P, 1024], F32, name="mix", tag="mix", bufs=5)
            prev = bank_s[pair][:].bitcast(BF16).rearrange("p (g k e) -> p g e k", g=4, e=2)
            gate = u_raw[pair][:].rearrange("p (g e k) -> p g e k", g=4, e=2)
            if pair < PAIRS - 1:
                nc.vector.tensor_tensor(out=t[:].rearrange("p (g e k) -> p g e k", g=4, e=2), in0=prev, in1=gate, op=ALU.mult)
            else:
                prev = bank_s[pair][:].bitcast(BF16).rearrange("p (b s k e) -> p s b e k", b=2, s=2, e=2)
                gate = u_raw[pair][:].rearrange("p (b s e k) -> p s b e k", b=2, s=2, e=2)
                for s in range(2):
                    nc.vector.tensor_tensor(
                        out=t[:, 512 * s : 512 * s + 512].rearrange("p (b e k) -> p b e k", b=2, e=2),
                        in0=prev[:, s],
                        in1=gate[:, s],
                        op=ALU.mult,
                    )
            mix[pair] = t

        def new_part(pair, lo=0, hi=1024):
            if not ok(pair):
                return
            c = cand[pair][:, lo:hi]
            nc.vector.scalar_tensor_tensor(out=c, in0=u_raw[pair][:, lo:hi], scalar=1.0, in1=c, op0=ALU.subtract, op1=ALU.mult)

        def new_tail(pair, half):
            c = cand[pair][:, 512 * half : 512 * half + 512].rearrange("p (b f) -> p b f", b=2)
            u_half = u_raw[pair][:].rearrange("p (b f) -> p b f", b=2)[:, :, 256 * half : 256 * half + 256]
            nc.vector.scalar_tensor_tensor(out=c, in0=u_half, scalar=1.0, in1=c, op0=ALU.subtract, op1=ALU.mult)

        def blend_g(pair):
            if not ok(pair) or pair >= PAIRS - 2:
                return
            t = mix[pair]
            cols = slice(1024 - columns(pair), 1024)
            nc.gpsimd.tensor_tensor(out=t[:, cols], in0=t[:, cols], in1=cand[pair][:, cols], op=ALU.subtract)

        def subtract(pair, lo, hi):
            t = mix[pair]
            nc.vector.tensor_tensor(out=t[:, lo:hi], in0=t[:, lo:hi], in1=cand[pair][:, lo:hi], op=ALU.subtract)

        def store(pair):
            return out[2 * pair : 2 * pair + 2].rearrange("b (p f) -> p b f", p=P)

        def blend_z(pair):
            if not ok(pair):
                return
            subtract(pair, 0, 1024 - columns(pair))
            nc.sync.dma_start(out=store(pair), in_=mix[pair][:].rearrange("p (b f) -> p b f", f=512))

        def blend_batch(pair, b):
            subtract(pair, 512 * b, 512 * b + 512)
            nc.sync.dma_start(out=store(pair)[:, b, :], in_=mix[pair][:, 512 * b : 512 * b + 512])

        def blend_tail(pair, half):
            subtract(pair, 512 * half, 512 * half + 512)
            nc.sync.dma_start(
                out=store(pair)[:, :, 256 * half : 256 * half + 256],
                in_=mix[pair][:, 512 * half : 512 * half + 512].rearrange("p (b f) -> p b f", b=2),
            )

        ident = const.tile([P, P], F32, name="ident")
        make_identity(nc, ident[:])
        warm = const.tile([P, 2], F32, name="warm")
        nc.vector.memset(warm[:], 0.0)
        nc.scalar.activation(out=warm[:, 1:2], in_=warm[:, 0:1], func=TANH)

        ck_raw = const.tile([P, 1024], BF16, name="ck_raw")
        ck_codes = const.tile([P, 512], U32, name="ck_codes", align_bytes=64)
        nc.gpsimd.memset(ck_codes[:].bitcast(I32), 0)
        ck_h = c_kernel[0:256, :].rearrange("(q t) u -> q (t u)", t=4)
        ck_c = c_kernel[256:512, :].rearrange("(i q h) u -> q i (h u)", i=2, h=2)

        def load_ck():
            nc.sync.dma_start(out=ck_raw[0:64, 0:512], in_=ck_h)
            nc.sync.dma_start(out=ck_raw[64:128, 0:512], in_=ck_h)
            nc.sync.dma_start(out=ck_raw[0:64, 512:1024].rearrange("q (i f) -> q i f", i=2), in_=ck_c)
            nc.sync.dma_start(out=ck_raw[64:128, 512:1024].rearrange("q (i f) -> q i f", i=2), in_=ck_c)

        sup_raw = []
        load_r(0)
        for i in range(2):
            t = const.tile([P, 2048], BF16, name="sup_raw%d" % i)
            sup_raw.append(t)
        for a in range(2):
            for t, sup in zip(sup_raw, (support0, support1)):
                nc.sync.dma_start(
                    out=t[:, 1024 * a : 1024 * a + 1024],
                    in_=sup.rearrange("(p a j) n -> p a (j n)", a=2, j=2)[:, a, :],
                )
        load_r(1)
        load_ck()
        load_h(0)
        load_s(0)
        load_u(0)
        load_r(2)
        load_h(1)
        load_s(1)
        load_s(2)
        load_u(1)

        def fetch(step):
            load_r(step + 1)
            load_h(step)
            load_s(step + 1)
            load_u(step)

        for step in range(2, FETCH):
            fetch(step)

        ck_grp = const.tile([P, 1024], BF16, name="ck_grp", align_bytes=64)
        ck_both = const.tile([P, 384], U32, name="ck_both", align_bytes=64)
        ck_scales = const.tile([P, 384], U8, name="ck_scales", align_bytes=64)
        sup_grp = const.tile([P, 4096], BF16, name="sup_grp", align_bytes=64)
        sup_codes = const.tile([P, 1024], U32, name="sup_codes", align_bytes=64)
        sup_scales = const.tile([P, 1024], U8, name="sup_scales", align_bytes=64)

        def prepare_kernel():
            nc.vector.tensor_copy(
                out=ck_grp[:].rearrange("p (v u t) -> p v u t", v=2, t=4),
                in_=ck_raw[:].rearrange("p (v t u) -> p v u t", v=2, t=4),
            )
            for v, lo in ((0, 0), (0, 128), (1, 256)):
                nc.vector.quantize_mx(
                    out=ck_both[:, lo : lo + 128].bitcast(FP8X4),
                    scales=ck_scales[:, lo : lo + 128],
                    in_=ck_grp[:, 512 * v : 512 * v + 512],
                )
            dst = ck_codes[:].bitcast(I32).rearrange("p (v s u) -> p v s u", v=2, s=2)
            codes = ck_both[:, 128:384].bitcast(I32).rearrange("p (v u) -> p v u", v=2)
            nc.vector.tensor_copy(out=dst[0:64, :, 0, :], in_=codes[0:64])
            nc.vector.tensor_copy(out=dst[64:128, :, 1, :], in_=codes[64:128])

        grp_words = sup_grp[:].bitcast(F32).rearrange("w (a b i f) -> w a b i f", a=2, b=2, i=2)

        def prepare_supports(a):
            for i in range(2):
                words = sup_raw[i][:].bitcast(F32)
                bank = psum.tile([P, 512], F32, name="bank_c", tag=("bank_x" if i == 0 else "bank_y"))
                for g in range(4):
                    col = 512 * a + 128 * g
                    nc.tensor.transpose(out=bank[:, 128 * g : 128 * g + 128], in_=words[:, col : col + 128], identity=ident[:])
                dst = grp_words[:, a, :, i, :].rearrange("w b (p t) -> w b p t", t=2)
                src = bank[:].rearrange("w (b t p) -> w b p t", b=2, t=2)
                if i == 0:
                    nc.vector.tensor_copy(out=dst, in_=src)
                else:
                    nc.scalar.copy(out=dst, in_=src)

        def quantise_supports(a):
            nc.vector.quantize_mx(
                out=sup_codes[:, 512 * a : 512 * a + 512].bitcast(FP8X4),
                scales=sup_scales[:, 512 * a : 512 * a + 512],
                in_=sup_grp[:, 2048 * a : 2048 * a + 2048],
            )

        tr_r(0)
        ev_r(0)
        q_r(0)
        prepare_supports(0)
        prepare_supports(1)
        quantise_supports(0)
        tr_r(1)
        ev_r(1)
        quantise_supports(1)
        q_r(1)
        mx1(0, 0)
        mx1(0, 1)
        ev_y(0, 0)
        ev_y(0, 1)
        prepare_kernel()
        tr_x(0, 0)
        tr_x(0, 1)
        ev_x(0, 0)
        ev_x(0, 1)
        q_x(0)
        tr_s(0)
        keep_part(0)
        mx1(0, 2)
        mx1(0, 3)
        ev_y(0, 2)
        ev_y(0, 3)
        fetch(FETCH)
        for step in range(1, PAIRS):
            last = step == PAIRS - 1
            q_y(step - 1)
            tr_r(step + 1)
            ev_r(step + 1)
            tr_x(step, 0)
            ev_x(step, 0)
            if step == 1:
                tr_s(1)
            mx1(step, 0)
            mx1(step, 1)
            mx2(step - 1, 0)
            ev_y(step, 0)
            ev_y(step, 1)
            tanh(step - 1, 0)
            new_part(step - 2)
            q_r(step + 1)
            blend_g(step - 2)
            tr_x(step, 1)
            tr_s(step + 1)
            keep_part(step)
            if helped(step):
                ev_x(step, 1)
            if not last:
                blend_z(step - 2)
            if not helped(step):
                ev_x(step, 1)
            mx1(step, 2)
            mx1(step, 3)
            mx2(step - 1, 1)
            ev_y(step, 2)
            ev_y(step, 3)
            tanh(step - 1, 1)
            if not last:
                q_x(step)
            fetch(step + FETCH)
        a, b = PAIRS - 2, PAIRS - 1
        q_x(b)
        q_y(b, 0, 2)
        new_part(a, 0, 512)
        mx2_tail(b, 0)
        tanh_tail(b, 0)
        q_y(b, 2, 4)
        blend_z(a - 1)
        blend_batch(a, 0)
        new_part(a, 512, 1024)
        mx2_tail(b, 1)
        tanh_tail(b, 1)
        new_tail(b, 0)
        new_tail(b, 1)
        blend_batch(a, 1)
        blend_tail(b, 0)
        blend_tail(b, 1)
